import numpy as np
import ml_dtypes


def mxq(x, axis, fmt="e4m3"):
    dtype, down = {"e4m3": (ml_dtypes.float8_e4m3fn, 7), "e5m2": (ml_dtypes.float8_e5m2, 14)}[fmt]
    v = np.moveaxis(np.asarray(x, np.float32).astype(ml_dtypes.bfloat16).astype(np.float64), axis, -1)
    blocks = v.reshape(v.shape[:-1] + (-1, 32))
    amax = np.abs(blocks).max(-1, keepdims=True)
    byte = np.maximum(np.where(amax > 0, np.frexp(amax)[1] - 1 + 127, 0) - down, 1)
    scale = np.exp2(byte - 127.0)
    codes = (blocks / scale).astype(np.float32).astype(dtype).astype(np.float64)
    return np.moveaxis((codes * scale).reshape(v.shape), -1, axis)


WIDE = False


def mx_kscale(k):
    if not WIDE:
        return np.ones(k)
    levels = np.array([10, -10, 5, -5, 0])
    if k % 512:
        return np.exp2(np.random.permutation(np.resize(levels, k // 32))).repeat(32)
    a = np.empty((k // 512, 16))
    for p in range(k // 512):
        a[p, :8] = np.random.permutation(np.resize(levels, 8))
        for g in range(8):
            far = levels[np.abs(levels - a[p, g]) >= 10]
            a[p, g + 8] = far[np.random.randint(len(far))]
    return np.exp2(a.ravel()).repeat(32)


BF16 = ml_dtypes.bfloat16


def bf(x):
    return np.asarray(x, np.float32).astype(BF16)


def f64(x):
    return np.asarray(x).astype(np.float64)


B, IN, H, OUT, L, STEPS = 4096, 512, 512, 128, 3, 3
LN_EPS = 1e-5


def layer_norm(v, g, b):
    m = v.mean(-1, keepdims=True)
    var = ((v - m) ** 2).mean(-1, keepdims=True)
    return (v - m) / np.sqrt(var + LN_EPS) * g + b


def setup_inputs():
    s = mx_kscale(H)
    s = s / s.max()
    return {"h": bf(np.random.standard_normal((B, H)) * s),
            "W_liq": bf(np.random.standard_normal((L, H, H)) / np.sqrt(H) / s),
            "b_liq": bf(np.random.standard_normal((L, H)) * 0.3),
            "g_liq": bf(1.0 + 0.1 * np.random.standard_normal((L, H))),
            "beta_liq": bf(np.random.standard_normal((L, H)) * 0.3)}


def reference(h, W_liq, b_liq, g_liq, beta_liq):
    h = f64(h)
    lin = mxq(h, 1, "e4m3") @ mxq(f64(W_liq), 2, "e4m3").transpose(0, 2, 1)
    pre = h[None] + lin + f64(b_liq)[:, None, :]
    return layer_norm(pre, f64(g_liq)[:, None, :], f64(beta_liq)[:, None, :]).sum(0)

@@ -1,0 +1,327 @@
+import concourse.mybir as mybir
+from concourse.masks import make_identity
+
+F32 = mybir.dt.float32
+BF16 = mybir.dt.bfloat16
+U32 = mybir.dt.uint32
+U8 = mybir.dt.uint8
+FP8X4 = mybir.dt.float8_e4m3fn_x4
+ALU = mybir.AluOpType
+ACT = mybir.ActivationFunctionType
+
+P = 128
+ROWS = 4096
+H = 512
+BRANCHES = 3
+TILES = ROWS // P
+CHUNKS = H // P
+QUAD = 4
+LOAD_TILES = 8
+UNITS = BRANCHES * CHUNKS
+UNITS_PER_STEP = UNITS // QUAD
+NORM_LAG = 2
+FLIP_LAG = QUAD - 1 + NORM_LAG + 1
+BACK_LAG = FLIP_LAG + QUAD
+STEPS = TILES + BACK_LAG
+LN_EPS = 1e-5
+
+FLOPS = 2 * ROWS * H * H * BRANCHES
+
+
+def transpose_words(nc, bank, column, words, ident):
+    for u in range(2):
+        nc.tensor.transpose(
+            bank[:, u, column : column + P], words[:, u : H // 2 : 2], ident[:]
+        )
+
+
+def tile_advancedliquidneuralnetwork_pa_t_kernel(
+    tc, h, W_liq, b_liq, g_liq, beta_liq, out
+):
+    nc = tc.nc
+    h_view = h.rearrange("(p j) k -> p j k", j=TILES)
+    out_view = out.rearrange("(p j) o -> p j o", j=TILES)
+
+    with tc.tile_pool(name="keep", bufs=1) as keep, tc.tile_pool(
+        name="pairs", bufs=2
+    ) as pairs, tc.tile_pool(name="triples", bufs=3) as triples, tc.tile_pool(
+        name="small", bufs=6
+    ) as small, tc.psum_pool(name="flip", bufs=2) as flip, tc.psum_pool(
+        name="prod", bufs=BRANCHES
+    ) as prod, tc.psum_pool(name="cols", bufs=UNITS_PER_STEP) as cols, tc.manual_schedule():
+        w_rows = keep.tile([P, UNITS, H], BF16)
+        h_rows = keep.tile([P, TILES, H], BF16)
+        w_view = W_liq.rearrange("l (c p) k -> p (l c) k", p=P)
+        nc.sync.dma_start(out=w_rows[:, 0:CHUNKS, :], in_=w_view[:, 0:CHUNKS, :])
+        nc.sync.dma_start(out=h_rows[:, 0:LOAD_TILES, :], in_=h_view[:, 0:LOAD_TILES, :])
+        nc.sync.dma_start(out=w_rows[:, CHUNKS:, :], in_=w_view[:, CHUNKS:, :])
+        for j0 in range(LOAD_TILES, TILES, LOAD_TILES):
+            nc.sync.dma_start(
+                out=h_rows[:, j0 : j0 + LOAD_TILES, :], in_=h_view[:, j0 : j0 + LOAD_TILES, :]
+            )
+        bias_all = keep.tile([P, BRANCHES, H], BF16)
+        nc.scalar.dma_start(
+            out=bias_all[:].rearrange("p l o -> p (l o)"),
+            in_=b_liq.rearrange("l o -> (l o)").partition_broadcast(P),
+        )
+        vec_rows = keep.tile([P, P], BF16)
+        nc.vector.memset(vec_rows[:], 0.0)
+        nc.scalar.dma_start(
+            out=vec_rows[0:UNITS, :], in_=g_liq.rearrange("l (c p) -> (l c) p", p=P)
+        )
+        nc.scalar.dma_start(
+            out=vec_rows[UNITS : 2 * UNITS, :], in_=beta_liq.rearrange("l (c p) -> (l c) p", p=P)
+        )
+
+        ident = keep.tile([P, P], F32)
+        make_identity(nc, ident[:])
+        eps = keep.tile([P, 1], F32)
+        nc.vector.memset(eps[:], LN_EPS)
+
+        w_words = w_rows[:].bitcast(F32)
+        w_codes = keep.tile([P, BRANCHES, H], U32, align_bytes=64)
+        w_scales = keep.tile([P, BRANCHES, H], U8, align_bytes=64)
+
+        def quantise_weights(l):
+            w_grouped = pairs.tile([P, H, 4], BF16, align_bytes=64)
+            w_grouped_words = w_grouped[:].bitcast(F32)
+            for half in range(2):
+                w_bank = flip.tile([P, 2, 2 * P], F32, tag="bank")
+                for c in range(2):
+                    transpose_words(
+                        nc, w_bank, c * P, w_words[:, l * CHUNKS + 2 * half + c, :], ident
+                    )
+                nc.scalar.copy(
+                    out=w_grouped_words[:, half * 2 * P : (half + 1) * 2 * P, :],
+                    in_=w_bank[:].rearrange("p u o -> p o u"),
+                )
+            nc.vector.quantize_mx(
+                out=w_codes[:, l, :].bitcast(FP8X4),
+                scales=w_scales[:, l, :],
+                in_=w_grouped[:].rearrange("p o t -> p (o t)"),
+            )
+
+        h_words = h_rows[:].bitcast(F32)
+        h_codes = keep.tile([P, TILES * P], U32, align_bytes=64)
+        h_scales = keep.tile([P, TILES * P], U8, align_bytes=64)
+
+        grouped = {}
+
+        def group_two_tiles(j0):
+            h_bank = flip.tile([P, 2, 2 * P], F32, tag="bank")
+            for c in range(2):
+                transpose_words(nc, h_bank, c * P, h_words[:, j0 + c, :], ident)
+            h_grouped = pairs.tile([P, 2 * P, 4], BF16, align_bytes=64)
+            nc.vector.tensor_copy(
+                out=h_grouped[:].bitcast(F32), in_=h_bank[:].rearrange("p u r -> p r u")
+            )
+            grouped[j0] = h_grouped
+
+        def quantise_two_tiles(j0):
+            nc.vector.quantize_mx(
+                out=h_codes[:, j0 * P : (j0 + 2) * P].bitcast(FP8X4),
+                scales=h_scales[:, j0 * P : (j0 + 2) * P],
+                in_=grouped[j0][:].rearrange("p r t -> p (r t)"),
+            )
+
+        products = {}
+        resids = {}
+        normed = {}
+        stats = {}
+        summed = {}
+        results = {}
+
+        def multiply(j):
+            resid = pairs.tile([P, BRANCHES, H], F32)
+            for l in range(BRANCHES):
+                nc.gpsimd.tensor_tensor(
+                    out=resid[:, l, :], in0=h_rows[:, j, :], in1=bias_all[:, l, :], op=ALU.add
+                )
+            resids[j] = resid
+            products[j] = []
+            for l in range(BRANCHES):
+                lin = prod.tile([P, H], F32)
+                nc.tensor.matmul_mx(
+                    out=lin[:],
+                    lhsT=h_codes[:, j * P : (j + 1) * P].bitcast(FP8X4),
+                    lhsT_scale=h_scales[:, j * P : (j + 1) * P],
+                    rhs=w_codes[:, l, :].bitcast(FP8X4),
+                    rhs_scale=w_scales[:, l, :],
+                    start=True,
+                    stop=True,
+                )
+                products[j].append(lin)
+
+        def add_residual(j):
+            if j % QUAD == 0:
+                normed_quad = triples.tile([P, QUAD, BRANCHES, H], F32)
+                normed[j // QUAD] = normed_quad
+            pre = normed[j // QUAD][:, j % QUAD, :, :]
+            row_sum = small.tile([P, BRANCHES], F32)
+            for l in range(BRANCHES):
+                nc.vector.scalar_tensor_tensor(
+                    out=pre[:, l, :],
+                    in0=products[j][l][:],
+                    scalar=0.0,
+                    in1=resids[j][:, l, :],
+                    op0=ALU.add,
+                    op1=ALU.add,
+                    accum_out=row_sum[:, l : l + 1],
+                )
+            stats[j] = {"row_sum": row_sum}
+
+        def deviation(j):
+            pre = normed[j // QUAD][:, j % QUAD, :, :]
+            neg_mean = small.tile([P, BRANCHES], F32)
+            nc.scalar.mul(out=neg_mean[:], in_=stats[j]["row_sum"][:], mul=-1.0 / H)
+            stats[j]["neg_mean"] = neg_mean
+            sq_sum = small.tile([P, BRANCHES], F32)
+            for l in range(BRANCHES):
+                squares = triples.tile([P, H], F32)
+                nc.scalar.activation(
+                    out=squares[:],
+                    in_=pre[:, l, :],
+                    func=ACT.Square,
+                    bias=stats[j]["neg_mean"][:, l : l + 1],
+                    scale=1.0,
+                    accum_out=sq_sum[:, l : l + 1],
+                )
+            inv_std = small.tile([P, BRANCHES], F32)
+            nc.scalar.activation(
+                out=inv_std[:],
+                in_=sq_sum[:],
+                func=ACT.Abs_reciprocal_sqrt,
+                bias=eps[:],
+                scale=1.0 / H,
+            )
+            stats[j]["inv_std"] = inv_std
+
+        def offsets(j):
+            offset = small.tile([P, BRANCHES], F32)
+            nc.gpsimd.tensor_tensor(
+                out=offset[:], in0=stats[j]["neg_mean"][:], in1=stats[j]["inv_std"][:], op=ALU.mult
+            )
+            stats[j]["offset"] = offset
+
+        def normalise_on_vector(j):
+            pre = normed[j // QUAD][:, j % QUAD, :, :]
+            for l in range(BRANCHES):
+                nc.vector.tensor_scalar(
+                    out=pre[:, l, :],
+                    in0=pre[:, l, :],
+                    scalar1=stats[j]["neg_mean"][:, l : l + 1],
+                    scalar2=stats[j]["inv_std"][:, l : l + 1],
+                    op0=ALU.add,
+                    op1=ALU.mult,
+                )
+
+        def normalise(j):
+            pre = normed[j // QUAD][:, j % QUAD, :, :]
+            for l in range(BRANCHES):
+                nc.scalar.activation(
+                    out=pre[:, l, :],
+                    in_=pre[:, l, :],
+                    func=ACT.Identity,
+                    bias=stats[j]["offset"][:, l : l + 1],
+                    scale=stats[j]["inv_std"][:, l : l + 1],
+                )
+
+        def gain_and_sum(s, unit):
+            l, c = unit // CHUNKS, unit % CHUNKS
+            if unit == 0:
+                summed_quad = pairs.tile([P, CHUNKS, QUAD * P], F32)
+                summed[s] = summed_quad
+            flipped = cols.tile([P, QUAD * P], F32)
+            for q in range(QUAD):
+                nc.tensor.transpose(
+                    flipped[:, q * P : (q + 1) * P],
+                    normed[s][:, q, l, c * P : (c + 1) * P],
+                    ident[:],
+                )
+            if l == 0:
+                nc.vector.tensor_scalar(
+                    out=summed[s][:, c, :],
+                    in0=flipped[:],
+                    scalar1=vec_cols[:, unit : unit + 1],
+                    scalar2=shift_cols[:, c : c + 1],
+                    op0=ALU.mult,
+                    op1=ALU.add,
+                )
+            else:
+                nc.vector.scalar_tensor_tensor(
+                    out=summed[s][:, c, :],
+                    in0=flipped[:],
+                    scalar=vec_cols[:, unit : unit + 1],
+                    in1=summed[s][:, c, :],
+                    op0=ALU.mult,
+                    op1=ALU.add,
+                )
+
+        def back_to_rows(s, q, scalar_is_idle):
+            if q == 0:
+                result = pairs.tile([P, QUAD, H], F32)
+                results[s] = result
+            back = flip.tile([P, H], F32, tag="bank")
+            for c in range(CHUNKS):
+                nc.tensor.transpose(
+                    back[:, c * P : (c + 1) * P], summed[s][:, c, q * P : (q + 1) * P], ident[:]
+                )
+            if q % 2 == 0 or scalar_is_idle:
+                nc.scalar.copy(out=results[s][:, q, :], in_=back[:])
+            else:
+                nc.vector.tensor_copy(out=results[s][:, q, :], in_=back[:])
+            nc.sync.dma_start(out=out_view[:, s * QUAD + q, :], in_=results[s][:, q, :])
+
+        quantise_weights(0)
+        group_two_tiles(0)
+        quantise_two_tiles(0)
+        quantise_weights(1)
+        quantise_weights(2)
+        multiply(0)
+
+        vec_rows_f32 = keep.tile([P, P], F32)
+        nc.vector.tensor_copy(out=vec_rows_f32[:], in_=vec_rows[:])
+        vec_bank = flip.tile([P, P], F32, tag="bank")
+        nc.tensor.transpose(vec_bank[:], vec_rows_f32[:], ident[:])
+        vec_cols = keep.tile([P, P], F32)
+        nc.vector.tensor_copy(out=vec_cols[:], in_=vec_bank[:])
+        shift_cols = keep.tile([P, CHUNKS], F32)
+        nc.vector.tensor_tensor(
+            out=shift_cols[:],
+            in0=vec_cols[:, UNITS : UNITS + CHUNKS],
+            in1=vec_cols[:, UNITS + CHUNKS : UNITS + 2 * CHUNKS],
+            op=ALU.add,
+        )
+        nc.vector.tensor_tensor(
+            out=shift_cols[:],
+            in0=shift_cols[:],
+            in1=vec_cols[:, UNITS + 2 * CHUNKS : UNITS + 3 * CHUNKS],
+            op=ALU.add,
+        )
+
+        for t in range(STEPS):
+            if QUAD <= t - NORM_LAG < TILES:
+                offsets(t - NORM_LAG)
+            if t % 2 == 1 and t + 1 < TILES:
+                quantise_two_tiles(t + 1)
+            if t < TILES:
+                add_residual(t)
+            if 0 <= t - FLIP_LAG < TILES:
+                for i in range(UNITS_PER_STEP):
+                    gain_and_sum(
+                        (t - FLIP_LAG) // QUAD, ((t - FLIP_LAG) % QUAD) * UNITS_PER_STEP + i
+                    )
+            if t + 1 < TILES:
+                multiply(t + 1)
+            if 0 <= t - 1 < TILES:
+                deviation(t - 1)
+            if 0 <= t - NORM_LAG < QUAD:
+                normalise_on_vector(t - NORM_LAG)
+            if QUAD <= t - NORM_LAG < TILES:
+                normalise(t - NORM_LAG)
+            if 0 <= t - BACK_LAG < TILES:
+                back_to_rows(
+                    (t - BACK_LAG) // QUAD, (t - BACK_LAG) % QUAD, t - NORM_LAG >= TILES
+                )
+            if t % 2 == 0 and t + 2 < TILES:
+                group_two_tiles(t + 2)

@@ -15,105 +15,124 @@ H = 512
 BRANCHES = 3
 TILES = ROWS // P
 CHUNKS = H // P
-QUAD = 4
-LOAD_TILES = 8
-UNITS = BRANCHES * CHUNKS
-UNITS_PER_STEP = UNITS // QUAD
-NORM_LAG = 2
-FLIP_LAG = QUAD - 1 + NORM_LAG + 1
-BACK_LAG = FLIP_LAG + QUAD
-STEPS = TILES + BACK_LAG
+TERMS = 3
 LN_EPS = 1e-5
+
+SCALE_LAG = 2
+TURN_LAG = 3
+LEFT_LAG = 4
+BACK_LAG = 5
+STEPS = TILES + BACK_LAG
 
 FLOPS = 2 * ROWS * H * H * BRANCHES
 
 
 def transpose_words(nc, bank, column, words, ident):
     for u in range(2):
-        nc.tensor.transpose(
-            bank[:, u, column : column + P], words[:, u : H // 2 : 2], ident[:]
-        )
+        nc.tensor.transpose(bank[:, u, column : column + P], words[:, u : H // 2 : 2], ident[:])
 
 
-def tile_advancedliquidneuralnetwork_pa_t_kernel(
-    tc, h, W_liq, b_liq, g_liq, beta_liq, out
-):
+def tile_advancedliquidneuralnetwork_pa_t_kernel(tc, h, W_liq, b_liq, g_liq, beta_liq, out):
     nc = tc.nc
     h_view = h.rearrange("(p j) k -> p j k", j=TILES)
     out_view = out.rearrange("(p j) o -> p j o", j=TILES)
 
     with tc.tile_pool(name="keep", bufs=1) as keep, tc.tile_pool(
         name="pairs", bufs=2
-    ) as pairs, tc.tile_pool(name="triples", bufs=3) as triples, tc.tile_pool(
+    ) as pairs, tc.tile_pool(name="quads", bufs=4) as quads, tc.tile_pool(
         name="small", bufs=6
-    ) as small, tc.psum_pool(name="flip", bufs=2) as flip, tc.psum_pool(
+    ) as small, tc.psum_pool(name="gain", bufs=1) as gain, tc.psum_pool(
+        name="flip", bufs=1
+    ) as flip, tc.psum_pool(name="turn", bufs=1) as turn, tc.psum_pool(
         name="prod", bufs=BRANCHES
-    ) as prod, tc.psum_pool(name="cols", bufs=UNITS_PER_STEP) as cols, tc.manual_schedule():
-        w_rows = keep.tile([P, UNITS, H], BF16)
+    ) as prod, tc.manual_schedule():
+        w_rows = keep.tile([P, BRANCHES * CHUNKS, H], BF16)
         h_rows = keep.tile([P, TILES, H], BF16)
         w_view = W_liq.rearrange("l (c p) k -> p (l c) k", p=P)
-        nc.sync.dma_start(out=w_rows[:, 0:CHUNKS, :], in_=w_view[:, 0:CHUNKS, :])
-        nc.sync.dma_start(out=h_rows[:, 0:LOAD_TILES, :], in_=h_view[:, 0:LOAD_TILES, :])
-        nc.sync.dma_start(out=w_rows[:, CHUNKS:, :], in_=w_view[:, CHUNKS:, :])
-        for j0 in range(LOAD_TILES, TILES, LOAD_TILES):
-            nc.sync.dma_start(
-                out=h_rows[:, j0 : j0 + LOAD_TILES, :], in_=h_view[:, j0 : j0 + LOAD_TILES, :]
-            )
+
+        def load_w(l):
+            cs = slice(l * CHUNKS, (l + 1) * CHUNKS)
+            nc.sync.dma_start(out=w_rows[:, cs, :], in_=w_view[:, cs, :])
+
+        def load_h(j0, j1):
+            nc.sync.dma_start(out=h_rows[:, j0:j1, :], in_=h_view[:, j0:j1, :])
+
+        load_h(0, 2)
+        load_w(0)
+        load_w(1)
+        load_w(2)
+        load_h(2, 8)
+        for j0 in range(8, TILES, 8):
+            load_h(j0, j0 + 8)
         bias_all = keep.tile([P, BRANCHES, H], BF16)
         nc.scalar.dma_start(
             out=bias_all[:].rearrange("p l o -> p (l o)"),
             in_=b_liq.rearrange("l o -> (l o)").partition_broadcast(P),
         )
-        vec_rows = keep.tile([P, P], BF16)
-        nc.vector.memset(vec_rows[:], 0.0)
+        right = keep.tile([P, H], BF16)
+        nc.vector.memset(right[:], 0.0)
+        for i in range(TERMS):
+            nc.scalar.dma_start(out=right[i * BRANCHES : (i + 1) * BRANCHES, :], in_=g_liq)
         nc.scalar.dma_start(
-            out=vec_rows[0:UNITS, :], in_=g_liq.rearrange("l (c p) -> (l c) p", p=P)
+            out=right[TERMS * BRANCHES : (TERMS + 1) * BRANCHES, :], in_=beta_liq
         )
-        nc.scalar.dma_start(
-            out=vec_rows[UNITS : 2 * UNITS, :], in_=beta_liq.rearrange("l (c p) -> (l c) p", p=P)
-        )
+        g_row = keep.tile([P, BRANCHES, H], BF16)
+        nc.vector.memset(g_row[:], 0.0)
+        nc.scalar.dma_start(out=g_row[0:1, :, :], in_=g_liq.unsqueeze(0))
 
         ident = keep.tile([P, P], F32)
         make_identity(nc, ident[:])
+        ident_bf = keep.tile([P, P], BF16)
+        nc.vector.tensor_copy(out=ident_bf[:], in_=ident[:])
+        ones = keep.tile([P, P], BF16)
+        nc.vector.memset(ones[:], 1.0)
         eps = keep.tile([P, 1], F32)
         nc.vector.memset(eps[:], LN_EPS)
+        left = keep.tile([P, 3, 2, P], BF16)
+        nc.vector.memset(left[:], 0.0)
+        nc.vector.memset(left[:, :, :, TERMS * BRANCHES : (TERMS + 1) * BRANCHES], 1.0)
 
         w_words = w_rows[:].bitcast(F32)
         w_codes = keep.tile([P, BRANCHES, H], U32, align_bytes=64)
         w_scales = keep.tile([P, BRANCHES, H], U8, align_bytes=64)
+        w_grouped = {}
 
-        def quantise_weights(l):
-            w_grouped = pairs.tile([P, H, 4], BF16, align_bytes=64)
-            w_grouped_words = w_grouped[:].bitcast(F32)
+        def group_weights(l):
+            grouped_l = pairs.tile([P, H, 4], BF16, align_bytes=64)
+            w_grouped[l] = grouped_l
+            grouped_words = grouped_l[:].bitcast(F32)
             for half in range(2):
-                w_bank = flip.tile([P, 2, 2 * P], F32, tag="bank")
+                lin = prod.tile([P, H], F32)
+                w_bank = lin[:].rearrange("p (u o) -> p u o", u=2)
                 for c in range(2):
                     transpose_words(
                         nc, w_bank, c * P, w_words[:, l * CHUNKS + 2 * half + c, :], ident
                     )
                 nc.scalar.copy(
-                    out=w_grouped_words[:, half * 2 * P : (half + 1) * 2 * P, :],
-                    in_=w_bank[:].rearrange("p u o -> p o u"),
+                    out=grouped_words[:, half * 2 * P : (half + 1) * 2 * P, :],
+                    in_=w_bank.rearrange("p u o -> p o u"),
                 )
+
+        def quantise_weights(l):
             nc.vector.quantize_mx(
                 out=w_codes[:, l, :].bitcast(FP8X4),
                 scales=w_scales[:, l, :],
-                in_=w_grouped[:].rearrange("p o t -> p (o t)"),
+                in_=w_grouped[l][:].rearrange("p o t -> p (o t)"),
             )
 
         h_words = h_rows[:].bitcast(F32)
         h_codes = keep.tile([P, TILES * P], U32, align_bytes=64)
         h_scales = keep.tile([P, TILES * P], U8, align_bytes=64)
-
         grouped = {}
 
         def group_two_tiles(j0):
-            h_bank = flip.tile([P, 2, 2 * P], F32, tag="bank")
+            bank = flip.tile([P, H], F32)
+            h_bank = bank[:].rearrange("p (u r) -> p u r", u=2)
             for c in range(2):
                 transpose_words(nc, h_bank, c * P, h_words[:, j0 + c, :], ident)
             h_grouped = pairs.tile([P, 2 * P, 4], BF16, align_bytes=64)
-            nc.vector.tensor_copy(
-                out=h_grouped[:].bitcast(F32), in_=h_bank[:].rearrange("p u r -> p r u")
+            nc.scalar.copy(
+                out=h_grouped[:].bitcast(F32), in_=h_bank.rearrange("p u r -> p r u")
             )
             grouped[j0] = h_grouped
 
@@ -126,18 +145,23 @@ def tile_advancedliquidneuralnetwork_pa_t_kernel(
 
         products = {}
         resids = {}
-        normed = {}
-        stats = {}
-        summed = {}
-        results = {}
+        pres = {}
+        row_sums = {}
+        neg_means = {}
+        inv_stds = {}
+        lefts = {}
+        sums = {}
+        turned = {}
 
-        def multiply(j):
-            resid = pairs.tile([P, BRANCHES, H], F32)
+        def residual(j):
+            resid = quads.tile([P, BRANCHES, H], F32)
             for l in range(BRANCHES):
                 nc.gpsimd.tensor_tensor(
                     out=resid[:, l, :], in0=h_rows[:, j, :], in1=bias_all[:, l, :], op=ALU.add
                 )
             resids[j] = resid
+
+        def multiply(j):
             products[j] = []
             for l in range(BRANCHES):
                 lin = prod.tile([P, H], F32)
@@ -153,10 +177,7 @@ def tile_advancedliquidneuralnetwork_pa_t_kernel(
                 products[j].append(lin)
 
         def add_residual(j):
-            if j % QUAD == 0:
-                normed_quad = triples.tile([P, QUAD, BRANCHES, H], F32)
-                normed[j // QUAD] = normed_quad
-            pre = normed[j // QUAD][:, j % QUAD, :, :]
+            pre = quads.tile([P, BRANCHES, H], F32)
             row_sum = small.tile([P, BRANCHES], F32)
             for l in range(BRANCHES):
                 nc.vector.scalar_tensor_tensor(
@@ -168,160 +189,157 @@ def tile_advancedliquidneuralnetwork_pa_t_kernel(
                     op1=ALU.add,
                     accum_out=row_sum[:, l : l + 1],
                 )
-            stats[j] = {"row_sum": row_sum}
+            pres[j] = pre
+            row_sums[j] = row_sum
 
         def deviation(j):
-            pre = normed[j // QUAD][:, j % QUAD, :, :]
-            neg_mean = small.tile([P, BRANCHES], F32)
-            nc.scalar.mul(out=neg_mean[:], in_=stats[j]["row_sum"][:], mul=-1.0 / H)
-            stats[j]["neg_mean"] = neg_mean
+            if j % 2 == 0:
+                neg_mean = small.tile([P, 2, BRANCHES], F32)
+                inv_std = small.tile([P, 2, BRANCHES], F32)
+                neg_means[j // 2] = neg_mean
+                inv_stds[j // 2] = inv_std
+            mine = neg_means[j // 2][:, j % 2, :]
+            nc.scalar.mul(out=mine, in_=row_sums[j][:], mul=-1.0 / H)
             sq_sum = small.tile([P, BRANCHES], F32)
             for l in range(BRANCHES):
-                squares = triples.tile([P, H], F32)
+                squares = pairs.tile([P, H], F32)
                 nc.scalar.activation(
                     out=squares[:],
-                    in_=pre[:, l, :],
+                    in_=pres[j][:, l, :],
                     func=ACT.Square,
-                    bias=stats[j]["neg_mean"][:, l : l + 1],
+                    bias=mine[:, l : l + 1],
                     scale=1.0,
                     accum_out=sq_sum[:, l : l + 1],
                 )
-            inv_std = small.tile([P, BRANCHES], F32)
             nc.scalar.activation(
-                out=inv_std[:],
+                out=inv_stds[j // 2][:, j % 2, :],
                 in_=sq_sum[:],
                 func=ACT.Abs_reciprocal_sqrt,
                 bias=eps[:],
                 scale=1.0 / H,
             )
-            stats[j]["inv_std"] = inv_std
 
-        def offsets(j):
-            offset = small.tile([P, BRANCHES], F32)
+        def offsets(pair):
+            slot = left[:, pair % 3, :, :]
+            offset = small.tile([P, 2, BRANCHES], F32)
+            rest = small.tile([P, 2, BRANCHES], F32)
             nc.gpsimd.tensor_tensor(
-                out=offset[:], in0=stats[j]["neg_mean"][:], in1=stats[j]["inv_std"][:], op=ALU.mult
+                out=offset[:], in0=neg_means[pair][:], in1=inv_stds[pair][:], op=ALU.mult
             )
-            stats[j]["offset"] = offset
+            nc.gpsimd.tensor_copy(out=slot[:, :, 0:3], in_=offset[:])
+            nc.gpsimd.tensor_tensor(
+                out=rest[:], in0=offset[:], in1=slot[:, :, 0:3], op=ALU.subtract
+            )
+            nc.gpsimd.tensor_copy(out=slot[:, :, 3:6], in_=rest[:])
+            nc.gpsimd.tensor_tensor(
+                out=slot[:, :, 6:9], in0=rest[:], in1=slot[:, :, 3:6], op=ALU.subtract
+            )
 
-        def normalise_on_vector(j):
-            pre = normed[j // QUAD][:, j % QUAD, :, :]
+        def turn_left(pair):
+            left_bank = flip.tile([P, 2 * P], BF16, tag="bank")
+            for i in range(2):
+                nc.tensor.transpose(
+                    left_bank[:, i * P : (i + 1) * P], left[:, pair % 3, i, :], ident_bf[:]
+                )
+            left_turned = pairs.tile([P, 2 * P], BF16)
+            nc.scalar.copy(out=left_turned[:], in_=left_bank[:])
+            lefts[pair] = left_turned
+
+        def scale_and_sum(j):
+            pre = pres[j]
             for l in range(BRANCHES):
-                nc.vector.tensor_scalar(
+                nc.vector.scalar_tensor_tensor(
                     out=pre[:, l, :],
                     in0=pre[:, l, :],
-                    scalar1=stats[j]["neg_mean"][:, l : l + 1],
-                    scalar2=stats[j]["inv_std"][:, l : l + 1],
-                    op0=ALU.add,
+                    scalar=inv_stds[j // 2][:, j % 2, l : l + 1],
+                    in1=gains[l],
+                    op0=ALU.mult,
                     op1=ALU.mult,
                 )
-
-        def normalise(j):
-            pre = normed[j // QUAD][:, j % QUAD, :, :]
+            total = turn.tile([P, H], F32)
             for l in range(BRANCHES):
-                nc.scalar.activation(
-                    out=pre[:, l, :],
-                    in_=pre[:, l, :],
-                    func=ACT.Identity,
-                    bias=stats[j]["offset"][:, l : l + 1],
-                    scale=stats[j]["inv_std"][:, l : l + 1],
-                )
+                for c in range(CHUNKS):
+                    nc.tensor.matmul(
+                        total[:, c * P : (c + 1) * P],
+                        lhsT=pre[:, l, c * P : (c + 1) * P],
+                        rhs=ident[:],
+                        is_transpose=True,
+                        start=(l == 0 and c == 0),
+                        stop=(l == BRANCHES - 1 and c == CHUNKS - 1),
+                    )
+            sums[j] = total
 
-        def gain_and_sum(s, unit):
-            l, c = unit // CHUNKS, unit % CHUNKS
-            if unit == 0:
-                summed_quad = pairs.tile([P, CHUNKS, QUAD * P], F32)
-                summed[s] = summed_quad
-            flipped = cols.tile([P, QUAD * P], F32)
-            for q in range(QUAD):
-                nc.tensor.transpose(
-                    flipped[:, q * P : (q + 1) * P],
-                    normed[s][:, q, l, c * P : (c + 1) * P],
-                    ident[:],
-                )
-            if l == 0:
-                nc.vector.tensor_scalar(
-                    out=summed[s][:, c, :],
-                    in0=flipped[:],
-                    scalar1=vec_cols[:, unit : unit + 1],
-                    scalar2=shift_cols[:, c : c + 1],
-                    op0=ALU.mult,
-                    op1=ALU.add,
-                )
-            else:
-                nc.vector.scalar_tensor_tensor(
-                    out=summed[s][:, c, :],
-                    in0=flipped[:],
-                    scalar=vec_cols[:, unit : unit + 1],
-                    in1=summed[s][:, c, :],
-                    op0=ALU.mult,
-                    op1=ALU.add,
-                )
+        def take_sum(j):
+            total_sb = quads.tile([P, H], F32)
+            nc.scalar.copy(out=total_sb[:], in_=sums[j][:])
+            turned[j] = total_sb
 
-        def back_to_rows(s, q, scalar_is_idle):
-            if q == 0:
-                result = pairs.tile([P, QUAD, H], F32)
-                results[s] = result
-            back = flip.tile([P, H], F32, tag="bank")
+        backs = {}
+
+        def turn_back(j):
+            back = turn.tile([P, H], F32)
+            nc.tensor.matmul(
+                back[:],
+                lhsT=lefts[j // 2][:, (j % 2) * P : (j % 2 + 1) * P],
+                rhs=right[:],
+                start=True,
+                stop=False,
+            )
             for c in range(CHUNKS):
-                nc.tensor.transpose(
-                    back[:, c * P : (c + 1) * P], summed[s][:, c, q * P : (q + 1) * P], ident[:]
+                nc.tensor.matmul(
+                    back[:, c * P : (c + 1) * P],
+                    lhsT=turned[j][:, c * P : (c + 1) * P],
+                    rhs=ident[:],
+                    is_transpose=True,
+                    start=False,
+                    stop=(c == CHUNKS - 1),
                 )
-            if q % 2 == 0 or scalar_is_idle:
-                nc.scalar.copy(out=results[s][:, q, :], in_=back[:])
-            else:
-                nc.vector.tensor_copy(out=results[s][:, q, :], in_=back[:])
-            nc.sync.dma_start(out=out_view[:, s * QUAD + q, :], in_=results[s][:, q, :])
+            backs[j] = back
 
-        quantise_weights(0)
+        def store(j):
+            result = quads.tile([P, H], F32)
+            nc.scalar.copy(out=result[:], in_=backs[j][:])
+            nc.sync.dma_start(out=out_view[:, j, :], in_=result[:])
+
+        residual(0)
+        residual(1)
         group_two_tiles(0)
         quantise_two_tiles(0)
+        group_weights(0)
+        quantise_weights(0)
+        group_weights(1)
         quantise_weights(1)
+        group_weights(2)
         quantise_weights(2)
         multiply(0)
-
-        vec_rows_f32 = keep.tile([P, P], F32)
-        nc.vector.tensor_copy(out=vec_rows_f32[:], in_=vec_rows[:])
-        vec_bank = flip.tile([P, P], F32, tag="bank")
-        nc.tensor.transpose(vec_bank[:], vec_rows_f32[:], ident[:])
-        vec_cols = keep.tile([P, P], F32)
-        nc.vector.tensor_copy(out=vec_cols[:], in_=vec_bank[:])
-        shift_cols = keep.tile([P, CHUNKS], F32)
-        nc.vector.tensor_tensor(
-            out=shift_cols[:],
-            in0=vec_cols[:, UNITS : UNITS + CHUNKS],
-            in1=vec_cols[:, UNITS + CHUNKS : UNITS + 2 * CHUNKS],
-            op=ALU.add,
-        )
-        nc.vector.tensor_tensor(
-            out=shift_cols[:],
-            in0=shift_cols[:],
-            in1=vec_cols[:, UNITS + 2 * CHUNKS : UNITS + 3 * CHUNKS],
-            op=ALU.add,
-        )
+        gain_a = gain.tile([P, 2, H], BF16)
+        gain_b = gain.tile([P, 2, H], BF16)
+        gains = [gain_a[:, 0, :], gain_a[:, 1, :], gain_b[:, 0, :]]
+        for l in range(BRANCHES):
+            nc.tensor.matmul(gains[l], lhsT=ones[:], rhs=g_row[:, l, :], start=True, stop=True)
 
         for t in range(STEPS):
-            if QUAD <= t - NORM_LAG < TILES:
-                offsets(t - NORM_LAG)
+            if 0 <= t - BACK_LAG < TILES:
+                turn_back(t - BACK_LAG)
             if t % 2 == 1 and t + 1 < TILES:
                 quantise_two_tiles(t + 1)
             if t < TILES:
                 add_residual(t)
-            if 0 <= t - FLIP_LAG < TILES:
-                for i in range(UNITS_PER_STEP):
-                    gain_and_sum(
-                        (t - FLIP_LAG) // QUAD, ((t - FLIP_LAG) % QUAD) * UNITS_PER_STEP + i
-                    )
             if t + 1 < TILES:
                 multiply(t + 1)
+            if t + 2 < TILES:
+                residual(t + 2)
             if 0 <= t - 1 < TILES:
                 deviation(t - 1)
-            if 0 <= t - NORM_LAG < QUAD:
-                normalise_on_vector(t - NORM_LAG)
-            if QUAD <= t - NORM_LAG < TILES:
-                normalise(t - NORM_LAG)
+            if 0 <= t - 1 < TILES and t % 2 == 0:
+                offsets((t - 1) // 2)
+            if 0 <= t - TURN_LAG < TILES:
+                take_sum(t - TURN_LAG)
+            if 0 <= t - SCALE_LAG < TILES:
+                scale_and_sum(t - SCALE_LAG)
             if 0 <= t - BACK_LAG < TILES:
-                back_to_rows(
-                    (t - BACK_LAG) // QUAD, (t - BACK_LAG) % QUAD, t - NORM_LAG >= TILES
-                )
+                store(t - BACK_LAG)
+            if t % 2 == 0 and 0 <= t - LEFT_LAG < TILES:
+                turn_left((t - LEFT_LAG) // 2)
             if t % 2 == 0 and t + 2 < TILES:
                 group_two_tiles(t + 2)

@@ -19,7 +19,7 @@ TERMS = 3
 LN_EPS = 1e-5
 
 SCALE_LAG = 2
-TURN_LAG = 3
+SUM_LAG = 3
 LEFT_LAG = 4
 BACK_LAG = 5
 STEPS = TILES + BACK_LAG
@@ -39,7 +39,7 @@ def tile_advancedliquidneuralnetwork_pa_t_kernel(tc, h, W_liq, b_liq, g_liq, bet
 
     with tc.tile_pool(name="keep", bufs=1) as keep, tc.tile_pool(
         name="pairs", bufs=2
-    ) as pairs, tc.tile_pool(name="quads", bufs=4) as quads, tc.tile_pool(
+    ) as pairs, tc.tile_pool(name="quads", bufs=4) as quads, tc.tile_pool(name="fives", bufs=5) as fives, tc.tile_pool(
         name="small", bufs=6
     ) as small, tc.psum_pool(name="gain", bufs=1) as gain, tc.psum_pool(
         name="flip", bufs=1
@@ -177,7 +177,7 @@ def tile_advancedliquidneuralnetwork_pa_t_kernel(tc, h, W_liq, b_liq, g_liq, bet
                 products[j].append(lin)
 
         def add_residual(j):
-            pre = quads.tile([P, BRANCHES, H], F32)
+            pre = fives.tile([P, BRANCHES, H], F32)
             row_sum = small.tile([P, BRANCHES], F32)
             for l in range(BRANCHES):
                 nc.vector.scalar_tensor_tensor(
@@ -245,7 +245,7 @@ def tile_advancedliquidneuralnetwork_pa_t_kernel(tc, h, W_liq, b_liq, g_liq, bet
             nc.scalar.copy(out=left_turned[:], in_=left_bank[:])
             lefts[pair] = left_turned
 
-        def scale_and_sum(j):
+        def scale(j):
             pre = pres[j]
             for l in range(BRANCHES):
                 nc.vector.scalar_tensor_tensor(
@@ -256,6 +256,9 @@ def tile_advancedliquidneuralnetwork_pa_t_kernel(tc, h, W_liq, b_liq, g_liq, bet
                     op0=ALU.mult,
                     op1=ALU.mult,
                 )
+
+        def sum_branches(j):
+            pre = pres[j]
             total = turn.tile([P, H], F32)
             for l in range(BRANCHES):
                 for c in range(CHUNKS):
@@ -312,6 +315,7 @@ def tile_advancedliquidneuralnetwork_pa_t_kernel(tc, h, W_liq, b_liq, g_liq, bet
         group_weights(2)
         quantise_weights(2)
         multiply(0)
+        group_two_tiles(2)
         gain_a = gain.tile([P, 2, H], BF16)
         gain_b = gain.tile([P, 2, H], BF16)
         gains = [gain_a[:, 0, :], gain_a[:, 1, :], gain_b[:, 0, :]]
@@ -319,8 +323,8 @@ def tile_advancedliquidneuralnetwork_pa_t_kernel(tc, h, W_liq, b_liq, g_liq, bet
             nc.tensor.matmul(gains[l], lhsT=ones[:], rhs=g_row[:, l, :], start=True, stop=True)
 
         for t in range(STEPS):
-            if 0 <= t - BACK_LAG < TILES:
-                turn_back(t - BACK_LAG)
+            if 0 <= t - SUM_LAG < TILES:
+                sum_branches(t - SUM_LAG)
             if t % 2 == 1 and t + 1 < TILES:
                 quantise_two_tiles(t + 1)
             if t < TILES:
@@ -333,13 +337,15 @@ def tile_advancedliquidneuralnetwork_pa_t_kernel(tc, h, W_liq, b_liq, g_liq, bet
                 deviation(t - 1)
             if 0 <= t - 1 < TILES and t % 2 == 0:
                 offsets((t - 1) // 2)
-            if 0 <= t - TURN_LAG < TILES:
-                take_sum(t - TURN_LAG)
+            if 0 <= t - SUM_LAG < TILES:
+                take_sum(t - SUM_LAG)
             if 0 <= t - SCALE_LAG < TILES:
-                scale_and_sum(t - SCALE_LAG)
+                scale(t - SCALE_LAG)
+            if 0 <= t - BACK_LAG < TILES:
+                turn_back(t - BACK_LAG)
             if 0 <= t - BACK_LAG < TILES:
                 store(t - BACK_LAG)
             if t % 2 == 0 and 0 <= t - LEFT_LAG < TILES:
                 turn_left((t - LEFT_LAG) // 2)
-            if t % 2 == 0 and t + 2 < TILES:
-                group_two_tiles(t + 2)
+            if t % 2 == 0 and t + 4 < TILES:
+                group_two_tiles(t + 4)

@@ -18,11 +18,11 @@ CHUNKS = H // P
 TERMS = 3
 LN_EPS = 1e-5
 
+QUAD = 4
 SCALE_LAG = 2
 SUM_LAG = 3
-LEFT_LAG = 4
-BACK_LAG = 5
-STEPS = TILES + BACK_LAG
+BACK_LAG = 7
+BATCHES = [(0, 4), (4, 8), (8, 16), (16, 24), (24, 32)]
 
 FLOPS = 2 * ROWS * H * H * BRANCHES
 
@@ -39,7 +39,7 @@ def tile_advancedliquidneuralnetwork_pa_t_kernel(tc, h, W_liq, b_liq, g_liq, bet
 
     with tc.tile_pool(name="keep", bufs=1) as keep, tc.tile_pool(
         name="pairs", bufs=2
-    ) as pairs, tc.tile_pool(name="quads", bufs=4) as quads, tc.tile_pool(name="fives", bufs=5) as fives, tc.tile_pool(
+    ) as pairs, tc.tile_pool(name="quads", bufs=4) as quads, tc.tile_pool(name="fives", bufs=5) as fives, tc.tile_pool(name="eights", bufs=8) as eights, tc.tile_pool(
         name="small", bufs=6
     ) as small, tc.psum_pool(name="gain", bufs=1) as gain, tc.psum_pool(
         name="flip", bufs=1
@@ -57,11 +57,11 @@ def tile_advancedliquidneuralnetwork_pa_t_kernel(tc, h, W_liq, b_liq, g_liq, bet
         def load_h(j0, j1):
             nc.sync.dma_start(out=h_rows[:, j0:j1, :], in_=h_view[:, j0:j1, :])
 
-        load_h(0, 2)
+        load_h(0, 4)
         load_w(0)
         load_w(1)
         load_w(2)
-        load_h(2, 8)
+        load_h(4, 8)
         for j0 in range(8, TILES, 8):
             load_h(j0, j0 + 8)
         bias_all = keep.tile([P, BRANCHES, H], BF16)
@@ -88,7 +88,7 @@ def tile_advancedliquidneuralnetwork_pa_t_kernel(tc, h, W_liq, b_liq, g_liq, bet
         nc.vector.memset(ones[:], 1.0)
         eps = keep.tile([P, 1], F32)
         nc.vector.memset(eps[:], LN_EPS)
-        left = keep.tile([P, 3, 2, P], BF16)
+        left = keep.tile([P, 2, QUAD, P], BF16)
         nc.vector.memset(left[:], 0.0)
         nc.vector.memset(left[:, :, :, TERMS * BRANCHES : (TERMS + 1) * BRANCHES], 1.0)
 
@@ -97,18 +97,26 @@ def tile_advancedliquidneuralnetwork_pa_t_kernel(tc, h, W_liq, b_liq, g_liq, bet
         w_scales = keep.tile([P, BRANCHES, H], U8, align_bytes=64)
         w_grouped = {}
 
-        def group_weights(l):
+        def group_weights(l, copies):
             grouped_l = pairs.tile([P, H, 4], BF16, align_bytes=64)
             w_grouped[l] = grouped_l
             grouped_words = grouped_l[:].bitcast(F32)
-            for half in range(2):
-                lin = prod.tile([P, H], F32)
-                w_bank = lin[:].rearrange("p (u o) -> p u o", u=2)
+            if l == 1:
+                banks = []
+                for half in range(2):
+                    lin = prod.tile([P, H], F32)
+                    banks.append(lin)
+            else:
+                total = turn.tile([P, H], F32)
+                back = turn.tile([P, H], F32)
+                banks = [total, back]
+            for half, bank in enumerate(banks):
+                w_bank = bank[:].rearrange("p (u o) -> p u o", u=2)
                 for c in range(2):
                     transpose_words(
                         nc, w_bank, c * P, w_words[:, l * CHUNKS + 2 * half + c, :], ident
                     )
-                nc.scalar.copy(
+                copies[half](
                     out=grouped_words[:, half * 2 * P : (half + 1) * 2 * P, :],
                     in_=w_bank.rearrange("p u o -> p o u"),
                 )
@@ -125,22 +133,27 @@ def tile_advancedliquidneuralnetwork_pa_t_kernel(tc, h, W_liq, b_liq, g_liq, bet
         h_scales = keep.tile([P, TILES * P], U8, align_bytes=64)
         grouped = {}
 
-        def group_two_tiles(j0):
+        def group_two_tiles(j0, copy):
+            batch = [b for b in BATCHES if b[0] <= j0 < b[1]][0]
+            if j0 == batch[0]:
+                h_grouped = pairs.tile([P, 8 * P, 4], BF16, align_bytes=64)
+                grouped[batch] = h_grouped
             bank = flip.tile([P, H], F32)
             h_bank = bank[:].rearrange("p (u r) -> p u r", u=2)
             for c in range(2):
                 transpose_words(nc, h_bank, c * P, h_words[:, j0 + c, :], ident)
-            h_grouped = pairs.tile([P, 2 * P, 4], BF16, align_bytes=64)
-            nc.scalar.copy(
-                out=h_grouped[:].bitcast(F32), in_=h_bank.rearrange("p u r -> p r u")
+            r0 = (j0 - batch[0]) * P
+            copy(
+                out=grouped[batch][:, r0 : r0 + 2 * P, :].bitcast(F32),
+                in_=h_bank.rearrange("p u r -> p r u"),
             )
-            grouped[j0] = h_grouped
 
-        def quantise_two_tiles(j0):
+        def quantise_batch(batch):
+            j0, j1 = batch
             nc.vector.quantize_mx(
-                out=h_codes[:, j0 * P : (j0 + 2) * P].bitcast(FP8X4),
-                scales=h_scales[:, j0 * P : (j0 + 2) * P],
-                in_=grouped[j0][:].rearrange("p r t -> p (r t)"),
+                out=h_codes[:, j0 * P : j1 * P].bitcast(FP8X4),
+                scales=h_scales[:, j0 * P : j1 * P],
+                in_=grouped[batch][:, 0 : (j1 - j0) * P, :].rearrange("p r t -> p (r t)"),
             )
 
         products = {}
@@ -149,56 +162,63 @@ def tile_advancedliquidneuralnetwork_pa_t_kernel(tc, h, W_liq, b_liq, g_liq, bet
         row_sums = {}
         neg_means = {}
         inv_stds = {}
+        offs = {}
+        rests = {}
         lefts = {}
         sums = {}
         turned = {}
 
         def residual(j):
             resid = quads.tile([P, BRANCHES, H], F32)
-            for l in range(BRANCHES):
+            step = 1 if j == 0 else BRANCHES
+            for l in range(0, BRANCHES, step):
                 nc.gpsimd.tensor_tensor(
-                    out=resid[:, l, :], in0=h_rows[:, j, :], in1=bias_all[:, l, :], op=ALU.add
+                    out=resid[:, l : l + step, :],
+                    in0=h_rows[:, j, :].unsqueeze(1).to_broadcast([P, step, H]),
+                    in1=bias_all[:, l : l + step, :],
+                    op=ALU.add,
                 )
             resids[j] = resid
 
-        def multiply(j):
-            products[j] = []
-            for l in range(BRANCHES):
-                lin = prod.tile([P, H], F32)
-                nc.tensor.matmul_mx(
-                    out=lin[:],
-                    lhsT=h_codes[:, j * P : (j + 1) * P].bitcast(FP8X4),
-                    lhsT_scale=h_scales[:, j * P : (j + 1) * P],
-                    rhs=w_codes[:, l, :].bitcast(FP8X4),
-                    rhs_scale=w_scales[:, l, :],
-                    start=True,
-                    stop=True,
-                )
-                products[j].append(lin)
+        def multiply(j, l):
+            lin = prod.tile([P, H], F32)
+            nc.tensor.matmul_mx(
+                out=lin[:],
+                lhsT=h_codes[:, j * P : (j + 1) * P].bitcast(FP8X4),
+                lhsT_scale=h_scales[:, j * P : (j + 1) * P],
+                rhs=w_codes[:, l, :].bitcast(FP8X4),
+                rhs_scale=w_scales[:, l, :],
+                start=True,
+                stop=True,
+            )
+            products[j, l] = lin
 
-        def add_residual(j):
-            pre = fives.tile([P, BRANCHES, H], F32)
-            row_sum = small.tile([P, BRANCHES], F32)
-            for l in range(BRANCHES):
-                nc.vector.scalar_tensor_tensor(
-                    out=pre[:, l, :],
-                    in0=products[j][l][:],
-                    scalar=0.0,
-                    in1=resids[j][:, l, :],
-                    op0=ALU.add,
-                    op1=ALU.add,
-                    accum_out=row_sum[:, l : l + 1],
-                )
-            pres[j] = pre
-            row_sums[j] = row_sum
+        def add_residual(j, l):
+            if l == 0:
+                pre = fives.tile([P, BRANCHES, H], F32)
+                row_sum = small.tile([P, BRANCHES], F32)
+                pres[j] = pre
+                row_sums[j] = row_sum
+            nc.vector.scalar_tensor_tensor(
+                out=pres[j][:, l, :],
+                in0=products[j, l][:],
+                scalar=0.0,
+                in1=resids[j][:, l, :],
+                op0=ALU.add,
+                op1=ALU.add,
+                accum_out=row_sums[j][:, l : l + 1],
+            )
 
         def deviation(j):
-            if j % 2 == 0:
-                neg_mean = small.tile([P, 2, BRANCHES], F32)
-                inv_std = small.tile([P, 2, BRANCHES], F32)
-                neg_means[j // 2] = neg_mean
-                inv_stds[j // 2] = inv_std
-            mine = neg_means[j // 2][:, j % 2, :]
+            s, q = j // QUAD, j % QUAD
+            if q == 0:
+                neg_mean = pairs.tile([P, QUAD, BRANCHES], F32)
+                inv_std = pairs.tile([P, QUAD, BRANCHES], F32)
+                offset = pairs.tile([P, QUAD, BRANCHES], F32)
+                neg_means[s] = neg_mean
+                inv_stds[s] = inv_std
+                offs[s] = offset
+            mine = neg_means[s][:, q, :]
             nc.scalar.mul(out=mine, in_=row_sums[j][:], mul=-1.0 / H)
             sq_sum = small.tile([P, BRANCHES], F32)
             for l in range(BRANCHES):
@@ -212,38 +232,48 @@ def tile_advancedliquidneuralnetwork_pa_t_kernel(tc, h, W_liq, b_liq, g_liq, bet
                     accum_out=sq_sum[:, l : l + 1],
                 )
             nc.scalar.activation(
-                out=inv_stds[j // 2][:, j % 2, :],
+                out=inv_stds[s][:, q, :],
                 in_=sq_sum[:],
                 func=ACT.Abs_reciprocal_sqrt,
                 bias=eps[:],
                 scale=1.0 / H,
             )
-
-        def offsets(pair):
-            slot = left[:, pair % 3, :, :]
-            offset = small.tile([P, 2, BRANCHES], F32)
-            rest = small.tile([P, 2, BRANCHES], F32)
-            nc.gpsimd.tensor_tensor(
-                out=offset[:], in0=neg_means[pair][:], in1=inv_stds[pair][:], op=ALU.mult
-            )
-            nc.gpsimd.tensor_copy(out=slot[:, :, 0:3], in_=offset[:])
-            nc.gpsimd.tensor_tensor(
-                out=rest[:], in0=offset[:], in1=slot[:, :, 0:3], op=ALU.subtract
-            )
-            nc.gpsimd.tensor_copy(out=slot[:, :, 3:6], in_=rest[:])
-            nc.gpsimd.tensor_tensor(
-                out=slot[:, :, 6:9], in0=rest[:], in1=slot[:, :, 3:6], op=ALU.subtract
-            )
-
-        def turn_left(pair):
-            left_bank = flip.tile([P, 2 * P], BF16, tag="bank")
-            for i in range(2):
-                nc.tensor.transpose(
-                    left_bank[:, i * P : (i + 1) * P], left[:, pair % 3, i, :], ident_bf[:]
+            for l in range(BRANCHES):
+                nc.scalar.activation(
+                    out=offs[s][:, q, l : l + 1],
+                    in_=mine[:, l : l + 1],
+                    func=ACT.Copy,
+                    scale=inv_stds[s][:, q, l : l + 1],
                 )
-            left_turned = pairs.tile([P, 2 * P], BF16)
+            if q == QUAD - 1:
+                nc.scalar.copy(out=left[:, s % 2, :, 0:3], in_=offs[s][:])
+
+        def second_term(s):
+            slot = left[:, s % 2, :, :]
+            rest = pairs.tile([P, QUAD, BRANCHES], F32)
+            rests[s] = rest
+            nc.vector.tensor_tensor(
+                out=rest[:], in0=offs[s][:], in1=slot[:, :, 0:3], op=ALU.subtract
+            )
+
+        def place_second_term(s):
+            nc.scalar.copy(out=left[:, s % 2, :, 3:6], in_=rests[s][:])
+
+        def third_term(s):
+            slot = left[:, s % 2, :, :]
+            nc.vector.tensor_tensor(
+                out=slot[:, :, 6:9], in0=rests[s][:], in1=slot[:, :, 3:6], op=ALU.subtract
+            )
+
+        def turn_left(s):
+            left_bank = flip.tile([P, QUAD * P], BF16, tag="bank")
+            for i in range(QUAD):
+                nc.tensor.transpose(
+                    left_bank[:, i * P : (i + 1) * P], left[:, s % 2, i, :], ident_bf[:]
+                )
+            left_turned = pairs.tile([P, QUAD * P], BF16)
             nc.scalar.copy(out=left_turned[:], in_=left_bank[:])
-            lefts[pair] = left_turned
+            lefts[s] = left_turned
 
         def scale(j):
             pre = pres[j]
@@ -251,7 +281,7 @@ def tile_advancedliquidneuralnetwork_pa_t_kernel(tc, h, W_liq, b_liq, g_liq, bet
                 nc.vector.scalar_tensor_tensor(
                     out=pre[:, l, :],
                     in0=pre[:, l, :],
-                    scalar=inv_stds[j // 2][:, j % 2, l : l + 1],
+                    scalar=inv_stds[j // QUAD][:, j % QUAD, l : l + 1],
                     in1=gains[l],
                     op0=ALU.mult,
                     op1=ALU.mult,
@@ -259,93 +289,144 @@ def tile_advancedliquidneuralnetwork_pa_t_kernel(tc, h, W_liq, b_liq, g_liq, bet
 
         def sum_branches(j):
             pre = pres[j]
-            total = turn.tile([P, H], F32)
+            if j < TILES - SUM_LAG:
+                total = turn.tile([P, H], F32)
+                bank = total
+            else:
+                lin = prod.tile([P, H], F32)
+                bank = lin
             for l in range(BRANCHES):
                 for c in range(CHUNKS):
                     nc.tensor.matmul(
-                        total[:, c * P : (c + 1) * P],
+                        bank[:, c * P : (c + 1) * P],
                         lhsT=pre[:, l, c * P : (c + 1) * P],
                         rhs=ident[:],
                         is_transpose=True,
                         start=(l == 0 and c == 0),
                         stop=(l == BRANCHES - 1 and c == CHUNKS - 1),
                     )
-            sums[j] = total
+            sums[j] = bank
 
-        def take_sum(j):
-            total_sb = quads.tile([P, H], F32)
-            nc.scalar.copy(out=total_sb[:], in_=sums[j][:])
+        def take_sum(j, copy):
+            total_sb = eights.tile([P, H], F32)
+            copy(out=total_sb[:], in_=sums[j][:])
             turned[j] = total_sb
 
         backs = {}
 
         def turn_back(j):
-            back = turn.tile([P, H], F32)
+            if j < TILES - BACK_LAG or j % 3 == 0:
+                back = turn.tile([P, H], F32)
+                bank = back
+            elif j % 3 == 1:
+                total = turn.tile([P, H], F32)
+                bank = total
+            else:
+                lin = prod.tile([P, H], F32)
+                bank = lin
             nc.tensor.matmul(
-                back[:],
-                lhsT=lefts[j // 2][:, (j % 2) * P : (j % 2 + 1) * P],
+                bank[:],
+                lhsT=lefts[j // QUAD][:, (j % QUAD) * P : (j % QUAD + 1) * P],
                 rhs=right[:],
                 start=True,
                 stop=False,
             )
             for c in range(CHUNKS):
                 nc.tensor.matmul(
-                    back[:, c * P : (c + 1) * P],
+                    bank[:, c * P : (c + 1) * P],
                     lhsT=turned[j][:, c * P : (c + 1) * P],
                     rhs=ident[:],
                     is_transpose=True,
                     start=False,
                     stop=(c == CHUNKS - 1),
                 )
-            backs[j] = back
+            backs[j] = bank
 
-        def store(j):
-            result = quads.tile([P, H], F32)
-            nc.scalar.copy(out=result[:], in_=backs[j][:])
+        def store(j, copy):
+            result = eights.tile([P, H], F32)
+            copy(out=result[:], in_=backs[j][:])
             nc.sync.dma_start(out=out_view[:, j, :], in_=result[:])
 
         residual(0)
         residual(1)
-        group_two_tiles(0)
-        quantise_two_tiles(0)
-        group_weights(0)
+        group_two_tiles(0, nc.vector.tensor_copy)
+        group_two_tiles(2, nc.scalar.copy)
+        group_weights(0, (nc.scalar.copy, nc.vector.tensor_copy))
+        quantise_batch(BATCHES[0])
         quantise_weights(0)
-        group_weights(1)
+        group_weights(1, (nc.scalar.copy, nc.scalar.copy))
+        multiply(0, 0)
         quantise_weights(1)
-        group_weights(2)
+        add_residual(0, 0)
+        group_weights(2, (nc.scalar.copy, nc.scalar.copy))
+        multiply(0, 1)
         quantise_weights(2)
-        multiply(0)
-        group_two_tiles(2)
+        add_residual(0, 1)
+        multiply(0, 2)
+        add_residual(0, 2)
         gain_a = gain.tile([P, 2, H], BF16)
         gain_b = gain.tile([P, 2, H], BF16)
         gains = [gain_a[:, 0, :], gain_a[:, 1, :], gain_b[:, 0, :]]
-        for l in range(BRANCHES):
-            nc.tensor.matmul(gains[l], lhsT=ones[:], rhs=g_row[:, l, :], start=True, stop=True)
 
-        for t in range(STEPS):
-            if 0 <= t - SUM_LAG < TILES:
+        for t in range(TILES):
+            if 0 <= t - SUM_LAG:
                 sum_branches(t - SUM_LAG)
-            if t % 2 == 1 and t + 1 < TILES:
-                quantise_two_tiles(t + 1)
-            if t < TILES:
-                add_residual(t)
+            if 1 <= t:
+                for l in range(BRANCHES):
+                    add_residual(t, l)
+            for batch in BATCHES[1:]:
+                if t == batch[0] - 1:
+                    quantise_batch(batch)
+            if t % QUAD == 2 and t >= 6:
+                third_term((t - 6) // QUAD)
+            if t % QUAD == 1 and t >= 5:
+                second_term((t - 5) // QUAD)
             if t + 1 < TILES:
-                multiply(t + 1)
+                for l in range(BRANCHES):
+                    multiply(t + 1, l)
+            if t == 0:
+                for l in range(BRANCHES):
+                    nc.tensor.matmul(
+                        gains[l], lhsT=ones[:], rhs=g_row[:, l, :], start=True, stop=True
+                    )
             if t + 2 < TILES:
                 residual(t + 2)
-            if 0 <= t - 1 < TILES:
+            if t >= 1:
                 deviation(t - 1)
-            if 0 <= t - 1 < TILES and t % 2 == 0:
-                offsets((t - 1) // 2)
-            if 0 <= t - SUM_LAG < TILES:
-                take_sum(t - SUM_LAG)
-            if 0 <= t - SCALE_LAG < TILES:
+            if SUM_LAG <= t < TILES - 1:
+                take_sum(t - SUM_LAG, nc.scalar.copy)
+            if t % QUAD == 1 and t >= 5:
+                place_second_term((t - 5) // QUAD)
+            if t >= SCALE_LAG:
                 scale(t - SCALE_LAG)
-            if 0 <= t - BACK_LAG < TILES:
+            if BACK_LAG <= t < TILES - 1:
                 turn_back(t - BACK_LAG)
-            if 0 <= t - BACK_LAG < TILES:
-                store(t - BACK_LAG)
-            if t % 2 == 0 and 0 <= t - LEFT_LAG < TILES:
-                turn_left((t - LEFT_LAG) // 2)
-            if t % 2 == 0 and t + 4 < TILES:
-                group_two_tiles(t + 4)
+                store(t - BACK_LAG, nc.scalar.copy)
+            if t % QUAD == 2 and t >= 6:
+                turn_left((t - 6) // QUAD)
+            for j0 in range(BATCHES[0][1], TILES, 2):
+                if t == max(j0 // 2 - 2, j0 - 8):
+                    group_two_tiles(j0, nc.scalar.copy)
+
+        last = TILES - 1
+        deviation(last)
+        sum_branches(last - 2)
+        scale(last - 1)
+        take_sum(last - 3, nc.scalar.copy)
+        take_sum(last - 2, nc.scalar.copy)
+        sum_branches(last - 1)
+        second_term(last // QUAD)
+        place_second_term(last // QUAD)
+        scale(last)
+        third_term(last // QUAD)
+        turn_back(last - 7)
+        turn_back(last - 6)
+        take_sum(last - 1, nc.scalar.copy)
+        sum_branches(last)
+        turn_left(last // QUAD)
+        store(last - 7, nc.vector.tensor_copy)
+        store(last - 6, nc.scalar.copy)
+        take_sum(last, nc.vector.tensor_copy)
+        for j in range(last - 5, TILES):
+            turn_back(j)
+            store(j, nc.vector.tensor_copy if j % 2 == 0 else nc.scalar.copy)

@@ -22,7 +22,9 @@ QUAD = 4
 SCALE_LAG = 2
 SUM_LAG = 3
 BACK_LAG = 7
-BATCHES = [(0, 4), (4, 8), (8, 16), (16, 24), (24, 32)]
+PASSES = (1, 1, 2)
+GROUPED = 4
+BATCHES = [(0, 2), (2, 4), (4, 8), (8, 16), (16, 24), (24, 32)]
 
 FLOPS = 2 * ROWS * H * H * BRANCHES
 
@@ -57,11 +59,11 @@ def tile_advancedliquidneuralnetwork_pa_t_kernel(tc, h, W_liq, b_liq, g_liq, bet
         def load_h(j0, j1):
             nc.sync.dma_start(out=h_rows[:, j0:j1, :], in_=h_view[:, j0:j1, :])
 
-        load_h(0, 4)
+        load_h(0, 2)
         load_w(0)
         load_w(1)
         load_w(2)
-        load_h(4, 8)
+        load_h(2, 8)
         for j0 in range(8, TILES, 8):
             load_h(j0, j0 + 8)
         bias_all = keep.tile([P, BRANCHES, H], BF16)
@@ -133,19 +135,24 @@ def tile_advancedliquidneuralnetwork_pa_t_kernel(tc, h, W_liq, b_liq, g_liq, bet
         h_scales = keep.tile([P, TILES * P], U8, align_bytes=64)
         grouped = {}
 
+        turned_words = {}
+
+        def flip_two_tiles(j0):
+            bank = flip.tile([P, H], F32)
+            h_bank = bank[:].rearrange("p (u r) -> p u r", u=2)
+            for c in range(2):
+                transpose_words(nc, h_bank, c * P, h_words[:, j0 + c, :], ident)
+            turned_words[j0] = h_bank
+
         def group_two_tiles(j0, copy):
             batch = [b for b in BATCHES if b[0] <= j0 < b[1]][0]
             if j0 == batch[0]:
                 h_grouped = pairs.tile([P, 8 * P, 4], BF16, align_bytes=64)
                 grouped[batch] = h_grouped
-            bank = flip.tile([P, H], F32)
-            h_bank = bank[:].rearrange("p (u r) -> p u r", u=2)
-            for c in range(2):
-                transpose_words(nc, h_bank, c * P, h_words[:, j0 + c, :], ident)
             r0 = (j0 - batch[0]) * P
             copy(
                 out=grouped[batch][:, r0 : r0 + 2 * P, :].bitcast(F32),
-                in_=h_bank.rearrange("p u r -> p r u"),
+                in_=turned_words[j0].rearrange("p u r -> p r u"),
             )
 
         def quantise_batch(batch):
@@ -170,7 +177,7 @@ def tile_advancedliquidneuralnetwork_pa_t_kernel(tc, h, W_liq, b_liq, g_liq, bet
 
         def residual(j):
             resid = quads.tile([P, BRANCHES, H], F32)
-            step = 1 if j == 0 else BRANCHES
+            step = 1 if j < 3 else BRANCHES
             for l in range(0, BRANCHES, step):
                 nc.gpsimd.tensor_tensor(
                     out=resid[:, l : l + step, :],
@@ -182,15 +189,16 @@ def tile_advancedliquidneuralnetwork_pa_t_kernel(tc, h, W_liq, b_liq, g_liq, bet
 
         def multiply(j, l):
             lin = prod.tile([P, H], F32)
-            nc.tensor.matmul_mx(
-                out=lin[:],
-                lhsT=h_codes[:, j * P : (j + 1) * P].bitcast(FP8X4),
-                lhsT_scale=h_scales[:, j * P : (j + 1) * P],
-                rhs=w_codes[:, l, :].bitcast(FP8X4),
-                rhs_scale=w_scales[:, l, :],
-                start=True,
-                stop=True,
-            )
+            for again in range(PASSES[l]):
+                nc.tensor.matmul_mx(
+                    out=lin[:],
+                    lhsT=h_codes[:, j * P : (j + 1) * P].bitcast(FP8X4),
+                    lhsT_scale=h_scales[:, j * P : (j + 1) * P],
+                    rhs=w_codes[:, l, :].bitcast(FP8X4),
+                    rhs_scale=w_scales[:, l, :],
+                    start=True,
+                    stop=True,
+                )
             products[j, l] = lin
 
         def add_residual(j, l):
@@ -275,17 +283,16 @@ def tile_advancedliquidneuralnetwork_pa_t_kernel(tc, h, W_liq, b_liq, g_liq, bet
             nc.scalar.copy(out=left_turned[:], in_=left_bank[:])
             lefts[s] = left_turned
 
-        def scale(j):
+        def scale(j, l):
             pre = pres[j]
-            for l in range(BRANCHES):
-                nc.vector.scalar_tensor_tensor(
-                    out=pre[:, l, :],
-                    in0=pre[:, l, :],
-                    scalar=inv_stds[j // QUAD][:, j % QUAD, l : l + 1],
-                    in1=gains[l],
-                    op0=ALU.mult,
-                    op1=ALU.mult,
-                )
+            nc.vector.scalar_tensor_tensor(
+                out=pre[:, l, :],
+                in0=pre[:, l, :],
+                scalar=inv_stds[j // QUAD][:, j % QUAD, l : l + 1],
+                in1=gains[l],
+                op0=ALU.mult,
+                op1=ALU.mult,
+            )
 
         def sum_branches(j):
             pre = pres[j]
@@ -349,19 +356,22 @@ def tile_advancedliquidneuralnetwork_pa_t_kernel(tc, h, W_liq, b_liq, g_liq, bet
 
         residual(0)
         residual(1)
+        flip_two_tiles(0)
         group_two_tiles(0, nc.vector.tensor_copy)
-        group_two_tiles(2, nc.scalar.copy)
         group_weights(0, (nc.scalar.copy, nc.vector.tensor_copy))
         quantise_batch(BATCHES[0])
         quantise_weights(0)
-        group_weights(1, (nc.scalar.copy, nc.scalar.copy))
+        group_weights(1, (nc.scalar.copy, nc.vector.tensor_copy))
         multiply(0, 0)
         quantise_weights(1)
         add_residual(0, 0)
-        group_weights(2, (nc.scalar.copy, nc.scalar.copy))
+        group_weights(2, (nc.scalar.copy, nc.vector.tensor_copy))
         multiply(0, 1)
         quantise_weights(2)
         add_residual(0, 1)
+        for j0 in range(2, GROUPED, 2):
+            flip_two_tiles(j0)
+            group_two_tiles(j0, nc.scalar.copy)
         multiply(0, 2)
         add_residual(0, 2)
         gain_a = gain.tile([P, 2, H], BF16)
@@ -369,26 +379,33 @@ def tile_advancedliquidneuralnetwork_pa_t_kernel(tc, h, W_liq, b_liq, g_liq, bet
         gains = [gain_a[:, 0, :], gain_a[:, 1, :], gain_b[:, 0, :]]
 
         for t in range(TILES):
-            if 0 <= t - SUM_LAG:
-                sum_branches(t - SUM_LAG)
-            if 1 <= t:
-                for l in range(BRANCHES):
+            for l in range(BRANCHES):
+                if t >= 1:
                     add_residual(t, l)
-            for batch in BATCHES[1:]:
-                if t == batch[0] - 1:
-                    quantise_batch(batch)
-            if t % QUAD == 2 and t >= 6:
-                third_term((t - 6) // QUAD)
-            if t % QUAD == 1 and t >= 5:
-                second_term((t - 5) // QUAD)
-            if t + 1 < TILES:
-                for l in range(BRANCHES):
+                if l == BRANCHES - 1:
+                    for batch in BATCHES[1:]:
+                        if t == max(batch[0] - 2, 0):
+                            quantise_batch(batch)
+                    if t % QUAD == 2 and t >= 6:
+                        third_term((t - 6) // QUAD)
+                    if t % QUAD == 1 and t >= 5:
+                        second_term((t - 5) // QUAD)
+                if t >= SCALE_LAG:
+                    scale(t - SCALE_LAG, l)
+                if t + 1 < TILES:
                     multiply(t + 1, l)
-            if t == 0:
-                for l in range(BRANCHES):
+                if t == 0:
                     nc.tensor.matmul(
                         gains[l], lhsT=ones[:], rhs=g_row[:, l, :], start=True, stop=True
                     )
+                if l == 0 and t >= SUM_LAG:
+                    sum_branches(t - SUM_LAG)
+                if l == 1:
+                    if BACK_LAG <= t < TILES - 1:
+                        turn_back(t - BACK_LAG)
+                    for j0 in range(GROUPED, TILES, 2):
+                        if t == max(j0 // 2 - 2, j0 - 9):
+                            flip_two_tiles(j0)
             if t + 2 < TILES:
                 residual(t + 2)
             if t >= 1:
@@ -397,27 +414,26 @@ def tile_advancedliquidneuralnetwork_pa_t_kernel(tc, h, W_liq, b_liq, g_liq, bet
                 take_sum(t - SUM_LAG, nc.scalar.copy)
             if t % QUAD == 1 and t >= 5:
                 place_second_term((t - 5) // QUAD)
-            if t >= SCALE_LAG:
-                scale(t - SCALE_LAG)
             if BACK_LAG <= t < TILES - 1:
-                turn_back(t - BACK_LAG)
                 store(t - BACK_LAG, nc.scalar.copy)
+            for j0 in range(GROUPED, TILES, 2):
+                if t == max(j0 // 2 - 2, j0 - 9):
+                    group_two_tiles(j0, nc.scalar.copy)
             if t % QUAD == 2 and t >= 6:
                 turn_left((t - 6) // QUAD)
-            for j0 in range(BATCHES[0][1], TILES, 2):
-                if t == max(j0 // 2 - 2, j0 - 8):
-                    group_two_tiles(j0, nc.scalar.copy)
 
         last = TILES - 1
         deviation(last)
         sum_branches(last - 2)
-        scale(last - 1)
+        for l in range(BRANCHES):
+            scale(last - 1, l)
         take_sum(last - 3, nc.scalar.copy)
         take_sum(last - 2, nc.scalar.copy)
         sum_branches(last - 1)
         second_term(last // QUAD)
         place_second_term(last // QUAD)
-        scale(last)
+        for l in range(BRANCHES):
+            scale(last, l)
         third_term(last // QUAD)
         turn_back(last - 7)
         turn_back(last - 6)

@@ -349,6 +349,34 @@ def tile_advancedliquidneuralnetwork_pa_t_kernel(tc, h, W_liq, b_liq, g_liq, bet
                 )
             backs[j] = bank
 
+        def add_branches(j):
+            direct = quads.tile([P, H], F32)
+            nc.vector.tensor_tensor(
+                out=direct[:], in0=pres[j][:, 0, :], in1=pres[j][:, 1, :], op=ALU.add
+            )
+            nc.vector.tensor_tensor(
+                out=direct[:], in0=direct[:], in1=pres[j][:, 2, :], op=ALU.add
+            )
+            turned[j] = direct
+
+        def correct(j):
+            lin = prod.tile([P, H], F32)
+            nc.tensor.matmul(
+                lin[:],
+                lhsT=lefts[j // QUAD][:, (j % QUAD) * P : (j % QUAD + 1) * P],
+                rhs=right[:],
+                start=True,
+                stop=True,
+            )
+            backs[j] = lin
+
+        def store_direct(j):
+            result = eights.tile([P, H], F32)
+            nc.vector.tensor_tensor(
+                out=result[:], in0=backs[j][:], in1=turned[j][:], op=ALU.add
+            )
+            nc.sync.dma_start(out=out_view[:, j, :], in_=result[:])
+
         def store(j, copy):
             result = eights.tile([P, H], F32)
             copy(out=result[:], in_=backs[j][:])
@@ -398,9 +426,9 @@ def tile_advancedliquidneuralnetwork_pa_t_kernel(tc, h, W_liq, b_liq, g_liq, bet
                     nc.tensor.matmul(
                         gains[l], lhsT=ones[:], rhs=g_row[:, l, :], start=True, stop=True
                     )
-                if l == 0 and t >= SUM_LAG:
-                    sum_branches(t - SUM_LAG)
-                if l == 1:
+                if l == 0:
+                    if t >= SUM_LAG:
+                        sum_branches(t - SUM_LAG)
                     if BACK_LAG <= t < TILES - 1:
                         turn_back(t - BACK_LAG)
                     for j0 in range(GROUPED, TILES, 2):
@@ -425,24 +453,31 @@ def tile_advancedliquidneuralnetwork_pa_t_kernel(tc, h, W_liq, b_liq, g_liq, bet
         last = TILES - 1
         deviation(last)
         sum_branches(last - 2)
+        take_sum(last - 3, nc.scalar.copy)
+        turn_back(last - 7)
         for l in range(BRANCHES):
             scale(last - 1, l)
-        take_sum(last - 3, nc.scalar.copy)
+        add_branches(last - 1)
         take_sum(last - 2, nc.scalar.copy)
-        sum_branches(last - 1)
+        turn_back(last - 6)
         second_term(last // QUAD)
         place_second_term(last // QUAD)
         for l in range(BRANCHES):
             scale(last, l)
         third_term(last // QUAD)
-        turn_back(last - 7)
-        turn_back(last - 6)
-        take_sum(last - 1, nc.scalar.copy)
-        sum_branches(last)
         turn_left(last // QUAD)
-        store(last - 7, nc.vector.tensor_copy)
+        add_branches(last)
+        store(last - 7, nc.scalar.copy)
         store(last - 6, nc.scalar.copy)
-        take_sum(last, nc.vector.tensor_copy)
-        for j in range(last - 5, TILES):
-            turn_back(j)
-            store(j, nc.vector.tensor_copy if j % 2 == 0 else nc.scalar.copy)
+        turn_back(last - 5)
+        turn_back(last - 4)
+        correct(last - 1)
+        correct(last)
+        store(last - 5, nc.scalar.copy)
+        store_direct(last - 1)
+        store_direct(last)
+        turn_back(last - 3)
+        store(last - 4, nc.scalar.copy)
+        turn_back(last - 2)
+        store(last - 3, nc.vector.tensor_copy)
+        store(last - 2, nc.scalar.copy)

@@ -22,7 +22,7 @@ QUAD = 4
 SCALE_LAG = 2
 SUM_LAG = 3
 BACK_LAG = 7
-PASSES = (1, 1, 2)
+PASSES = (2, 1, 1)
 GROUPED = 4
 BATCHES = [(0, 2), (2, 4), (4, 8), (8, 16), (16, 24), (24, 32)]
 
@@ -93,6 +93,9 @@ def tile_advancedliquidneuralnetwork_pa_t_kernel(tc, h, W_liq, b_liq, g_liq, bet
         left = keep.tile([P, 2, QUAD, P], BF16)
         nc.vector.memset(left[:], 0.0)
         nc.vector.memset(left[:, :, :, TERMS * BRANCHES : (TERMS + 1) * BRANCHES], 1.0)
+
+        first = keep.tile([P, 1], F32)
+        nc.scalar.activation(out=first[:], in_=eps[:], func=ACT.Abs_reciprocal_sqrt)
 
         w_words = w_rows[:].bitcast(F32)
         w_codes = keep.tile([P, BRANCHES, H], U32, align_bytes=64)
@@ -294,25 +297,25 @@ def tile_advancedliquidneuralnetwork_pa_t_kernel(tc, h, W_liq, b_liq, g_liq, bet
                 op1=ALU.mult,
             )
 
-        def sum_branches(j):
+        def sum_branches(j, branches):
             pre = pres[j]
-            if j < TILES - SUM_LAG:
-                total = turn.tile([P, H], F32)
-                bank = total
-            else:
-                lin = prod.tile([P, H], F32)
-                bank = lin
-            for l in range(BRANCHES):
+            if 0 in branches:
+                if j < TILES - SUM_LAG:
+                    total = turn.tile([P, H], F32)
+                    sums[j] = total
+                else:
+                    lin = prod.tile([P, H], F32)
+                    sums[j] = lin
+            for l in branches:
                 for c in range(CHUNKS):
                     nc.tensor.matmul(
-                        bank[:, c * P : (c + 1) * P],
+                        sums[j][:, c * P : (c + 1) * P],
                         lhsT=pre[:, l, c * P : (c + 1) * P],
                         rhs=ident[:],
                         is_transpose=True,
                         start=(l == 0 and c == 0),
                         stop=(l == BRANCHES - 1 and c == CHUNKS - 1),
                     )
-            sums[j] = bank
 
         def take_sum(j, copy):
             total_sb = eights.tile([P, H], F32)
@@ -428,7 +431,7 @@ def tile_advancedliquidneuralnetwork_pa_t_kernel(tc, h, W_liq, b_liq, g_liq, bet
                     )
                 if l == 0:
                     if t >= SUM_LAG:
-                        sum_branches(t - SUM_LAG)
+                        sum_branches(t - SUM_LAG, range(BRANCHES))
                     if BACK_LAG <= t < TILES - 1:
                         turn_back(t - BACK_LAG)
                     for j0 in range(GROUPED, TILES, 2):
@@ -452,7 +455,7 @@ def tile_advancedliquidneuralnetwork_pa_t_kernel(tc, h, W_liq, b_liq, g_liq, bet
 
         last = TILES - 1
         deviation(last)
-        sum_branches(last - 2)
+        sum_branches(last - 2, range(BRANCHES))
         take_sum(last - 3, nc.scalar.copy)
         turn_back(last - 7)
         for l in range(BRANCHES):

@@ -21,7 +21,7 @@ LN_EPS = 1e-5
 QUAD = 4
 SCALE_LAG = 2
 SUM_LAG = 3
-BACK_LAG = 7
+BACK_LAG = 8
 PASSES = (2, 1, 1)
 GROUPED = 4
 BATCHES = [(0, 2), (2, 4), (4, 8), (8, 16), (16, 24), (24, 32)]
@@ -41,7 +41,7 @@ def tile_advancedliquidneuralnetwork_pa_t_kernel(tc, h, W_liq, b_liq, g_liq, bet
 
     with tc.tile_pool(name="keep", bufs=1) as keep, tc.tile_pool(
         name="pairs", bufs=2
-    ) as pairs, tc.tile_pool(name="quads", bufs=4) as quads, tc.tile_pool(name="fives", bufs=5) as fives, tc.tile_pool(name="eights", bufs=8) as eights, tc.tile_pool(
+    ) as pairs, tc.tile_pool(name="quads", bufs=4) as quads, tc.tile_pool(name="fives", bufs=5) as fives, tc.tile_pool(name="triples", bufs=3) as triples, tc.tile_pool(name="eights", bufs=8) as eights, tc.tile_pool(
         name="small", bufs=6
     ) as small, tc.psum_pool(name="gain", bufs=1) as gain, tc.psum_pool(
         name="flip", bufs=1
@@ -71,12 +71,12 @@ def tile_advancedliquidneuralnetwork_pa_t_kernel(tc, h, W_liq, b_liq, g_liq, bet
             out=bias_all[:].rearrange("p l o -> p (l o)"),
             in_=b_liq.rearrange("l o -> (l o)").partition_broadcast(P),
         )
-        right = keep.tile([P, H], BF16)
-        nc.vector.memset(right[:], 0.0)
+        right_rows = keep.tile([P, H], BF16)
+        nc.vector.memset(right_rows[:], 0.0)
         for i in range(TERMS):
-            nc.scalar.dma_start(out=right[i * BRANCHES : (i + 1) * BRANCHES, :], in_=g_liq)
+            nc.scalar.dma_start(out=right_rows[i * BRANCHES : (i + 1) * BRANCHES, :], in_=g_liq)
         nc.scalar.dma_start(
-            out=right[TERMS * BRANCHES : (TERMS + 1) * BRANCHES, :], in_=beta_liq
+            out=right_rows[TERMS * BRANCHES : (TERMS + 1) * BRANCHES, :], in_=beta_liq
         )
         g_row = keep.tile([P, BRANCHES, H], BF16)
         nc.vector.memset(g_row[:], 0.0)
@@ -92,7 +92,7 @@ def tile_advancedliquidneuralnetwork_pa_t_kernel(tc, h, W_liq, b_liq, g_liq, bet
         nc.vector.memset(eps[:], LN_EPS)
         left = keep.tile([P, 2, QUAD, P], BF16)
         nc.vector.memset(left[:], 0.0)
-        nc.vector.memset(left[:, :, :, TERMS * BRANCHES : (TERMS + 1) * BRANCHES], 1.0)
+        nc.vector.memset(left[:, :, :, TERMS * BRANCHES : (TERMS + 1) * BRANCHES], -1.0 * H)
 
         first = keep.tile([P, 1], F32)
         nc.scalar.activation(out=first[:], in_=eps[:], func=ACT.Abs_reciprocal_sqrt)
@@ -170,7 +170,7 @@ def tile_advancedliquidneuralnetwork_pa_t_kernel(tc, h, W_liq, b_liq, g_liq, bet
         resids = {}
         pres = {}
         row_sums = {}
-        neg_means = {}
+        sq_sums = {}
         inv_stds = {}
         offs = {}
         rests = {}
@@ -205,11 +205,13 @@ def tile_advancedliquidneuralnetwork_pa_t_kernel(tc, h, W_liq, b_liq, g_liq, bet
             products[j, l] = lin
 
         def add_residual(j, l):
+            s, q = j // QUAD, j % QUAD
             if l == 0:
                 pre = fives.tile([P, BRANCHES, H], F32)
-                row_sum = small.tile([P, BRANCHES], F32)
                 pres[j] = pre
-                row_sums[j] = row_sum
+                if q == 0:
+                    row_sum = triples.tile([P, QUAD, BRANCHES], F32)
+                    row_sums[s] = row_sum
             nc.vector.scalar_tensor_tensor(
                 out=pres[j][:, l, :],
                 in0=products[j, l][:],
@@ -217,20 +219,14 @@ def tile_advancedliquidneuralnetwork_pa_t_kernel(tc, h, W_liq, b_liq, g_liq, bet
                 in1=resids[j][:, l, :],
                 op0=ALU.add,
                 op1=ALU.add,
-                accum_out=row_sums[j][:, l : l + 1],
+                accum_out=row_sums[s][:, q, l : l + 1],
             )
 
         def deviation(j):
             s, q = j // QUAD, j % QUAD
             if q == 0:
-                neg_mean = pairs.tile([P, QUAD, BRANCHES], F32)
                 inv_std = pairs.tile([P, QUAD, BRANCHES], F32)
-                offset = pairs.tile([P, QUAD, BRANCHES], F32)
-                neg_means[s] = neg_mean
                 inv_stds[s] = inv_std
-                offs[s] = offset
-            mine = neg_means[s][:, q, :]
-            nc.scalar.mul(out=mine, in_=row_sums[j][:], mul=-1.0 / H)
             sq_sum = small.tile([P, BRANCHES], F32)
             for l in range(BRANCHES):
                 squares = pairs.tile([P, H], F32)
@@ -238,26 +234,31 @@ def tile_advancedliquidneuralnetwork_pa_t_kernel(tc, h, W_liq, b_liq, g_liq, bet
                     out=squares[:],
                     in_=pres[j][:, l, :],
                     func=ACT.Square,
-                    bias=mine[:, l : l + 1],
-                    scale=1.0,
+                    bias=row_sums[s][:, q, l : l + 1],
+                    scale=-1.0 * H,
                     accum_out=sq_sum[:, l : l + 1],
                 )
+            sq_sums[j] = sq_sum
+
+        def inverse(j):
+            s, q = j // QUAD, j % QUAD
             nc.scalar.activation(
                 out=inv_stds[s][:, q, :],
-                in_=sq_sum[:],
+                in_=sq_sums[j][:],
                 func=ACT.Abs_reciprocal_sqrt,
                 bias=eps[:],
-                scale=1.0 / H,
+                scale=1.0 / H**3,
             )
-            for l in range(BRANCHES):
-                nc.scalar.activation(
-                    out=offs[s][:, q, l : l + 1],
-                    in_=mine[:, l : l + 1],
-                    func=ACT.Copy,
-                    scale=inv_stds[s][:, q, l : l + 1],
-                )
-            if q == QUAD - 1:
-                nc.scalar.copy(out=left[:, s % 2, :, 0:3], in_=offs[s][:])
+
+        def first_term(s):
+            offset = pairs.tile([P, QUAD, BRANCHES], F32)
+            offs[s] = offset
+            nc.vector.tensor_tensor(
+                out=offset[:], in0=row_sums[s][:], in1=inv_stds[s][:], op=ALU.mult
+            )
+
+        def place_first_term(s):
+            nc.scalar.copy(out=left[:, s % 2, :, 0:3], in_=offs[s][:])
 
         def second_term(s):
             slot = left[:, s % 2, :, :]
@@ -405,6 +406,10 @@ def tile_advancedliquidneuralnetwork_pa_t_kernel(tc, h, W_liq, b_liq, g_liq, bet
             group_two_tiles(j0, nc.scalar.copy)
         multiply(0, 2)
         add_residual(0, 2)
+        right = keep.tile([P, H], BF16)
+        nc.vector.tensor_scalar(
+            out=right[:], in0=right_rows[:], scalar1=-1.0 / H, scalar2=None, op0=ALU.mult
+        )
         gain_a = gain.tile([P, 2, H], BF16)
         gain_b = gain.tile([P, 2, H], BF16)
         gains = [gain_a[:, 0, :], gain_a[:, 1, :], gain_b[:, 0, :]]
@@ -417,10 +422,12 @@ def tile_advancedliquidneuralnetwork_pa_t_kernel(tc, h, W_liq, b_liq, g_liq, bet
                     for batch in BATCHES[1:]:
                         if t == max(batch[0] - 2, 0):
                             quantise_batch(batch)
-                    if t % QUAD == 2 and t >= 6:
-                        third_term((t - 6) // QUAD)
-                    if t % QUAD == 1 and t >= 5:
-                        second_term((t - 5) // QUAD)
+                    if t % QUAD == 1 and t > QUAD:
+                        first_term(t // QUAD - 1)
+                    if t % QUAD == 2 and t > QUAD:
+                        second_term(t // QUAD - 1)
+                    if t % QUAD == 3 and t > QUAD:
+                        third_term(t // QUAD - 1)
                 if t >= SCALE_LAG:
                     scale(t - SCALE_LAG, l)
                 if t + 1 < TILES:
@@ -432,7 +439,7 @@ def tile_advancedliquidneuralnetwork_pa_t_kernel(tc, h, W_liq, b_liq, g_liq, bet
                 if l == 0:
                     if t >= SUM_LAG:
                         sum_branches(t - SUM_LAG, range(BRANCHES))
-                    if BACK_LAG <= t < TILES - 1:
+                    if t >= BACK_LAG:
                         turn_back(t - BACK_LAG)
                     for j0 in range(GROUPED, TILES, 2):
                         if t == max(j0 // 2 - 2, j0 - 9):
@@ -443,26 +450,33 @@ def tile_advancedliquidneuralnetwork_pa_t_kernel(tc, h, W_liq, b_liq, g_liq, bet
                 deviation(t - 1)
             if SUM_LAG <= t < TILES - 1:
                 take_sum(t - SUM_LAG, nc.scalar.copy)
-            if t % QUAD == 1 and t >= 5:
-                place_second_term((t - 5) // QUAD)
-            if BACK_LAG <= t < TILES - 1:
+            if t >= 1:
+                inverse(t - 1)
+            if t % QUAD == 1 and t > QUAD:
+                place_first_term(t // QUAD - 1)
+            if t % QUAD == 2 and t > QUAD:
+                place_second_term(t // QUAD - 1)
+            if t >= BACK_LAG:
                 store(t - BACK_LAG, nc.scalar.copy)
             for j0 in range(GROUPED, TILES, 2):
                 if t == max(j0 // 2 - 2, j0 - 9):
                     group_two_tiles(j0, nc.scalar.copy)
-            if t % QUAD == 2 and t >= 6:
-                turn_left((t - 6) // QUAD)
+            if t % QUAD == 3 and t > QUAD:
+                turn_left(t // QUAD - 1)
 
         last = TILES - 1
         deviation(last)
         sum_branches(last - 2, range(BRANCHES))
         take_sum(last - 3, nc.scalar.copy)
+        inverse(last)
         turn_back(last - 7)
         for l in range(BRANCHES):
             scale(last - 1, l)
         add_branches(last - 1)
         take_sum(last - 2, nc.scalar.copy)
         turn_back(last - 6)
+        first_term(last // QUAD)
+        place_first_term(last // QUAD)
         second_term(last // QUAD)
         place_second_term(last // QUAD)
         for l in range(BRANCHES):

import concourse.mybir as mybir
from concourse.masks import make_identity

F32 = mybir.dt.float32
BF16 = mybir.dt.bfloat16
U32 = mybir.dt.uint32
U8 = mybir.dt.uint8
FP8X4 = mybir.dt.float8_e4m3fn_x4
ALU = mybir.AluOpType
ACT = mybir.ActivationFunctionType

P = 128
ROWS = 4096
H = 512
BRANCHES = 3
TILES = ROWS // P
CHUNKS = H // P
TERMS = 3
LN_EPS = 1e-5

QUAD = 4
SCALE_LAG = 2
SUM_LAG = 3
BACK_LAG = 8
PASSES = (2, 1, 1)
GROUPED = 4
BATCHES = [(0, 2), (2, 4), (4, 8), (8, 16), (16, 24), (24, 32)]

FLOPS = 2 * ROWS * H * H * BRANCHES


def transpose_words(nc, bank, column, words, ident):
    for u in range(2):
        nc.tensor.transpose(bank[:, u, column : column + P], words[:, u : H // 2 : 2], ident[:])


def tile_advancedliquidneuralnetwork_pa_t_kernel(tc, h, W_liq, b_liq, g_liq, beta_liq, out):
    nc = tc.nc
    h_view = h.rearrange("(p j) k -> p j k", j=TILES)
    out_view = out.rearrange("(p j) o -> p j o", j=TILES)

    with tc.tile_pool(name="keep", bufs=1) as keep, tc.tile_pool(
        name="pairs", bufs=2
    ) as pairs, tc.tile_pool(name="quads", bufs=4) as quads, tc.tile_pool(name="fives", bufs=5) as fives, tc.tile_pool(name="triples", bufs=3) as triples, tc.tile_pool(name="eights", bufs=8) as eights, tc.tile_pool(
        name="small", bufs=6
    ) as small, tc.psum_pool(name="gain", bufs=1) as gain, tc.psum_pool(
        name="flip", bufs=1
    ) as flip, tc.psum_pool(name="turn", bufs=1) as turn, tc.psum_pool(
        name="prod", bufs=BRANCHES
    ) as prod, tc.manual_schedule():
        w_rows = keep.tile([P, BRANCHES * CHUNKS, H], BF16)
        h_rows = keep.tile([P, TILES, H], BF16)
        w_view = W_liq.rearrange("l (c p) k -> p (l c) k", p=P)

        def load_w(l):
            cs = slice(l * CHUNKS, (l + 1) * CHUNKS)
            nc.sync.dma_start(out=w_rows[:, cs, :], in_=w_view[:, cs, :])

        def load_h(j0, j1):
            nc.sync.dma_start(out=h_rows[:, j0:j1, :], in_=h_view[:, j0:j1, :])

        load_h(0, 2)
        load_w(0)
        load_w(1)
        load_w(2)
        load_h(2, 8)
        for j0 in range(8, TILES, 8):
            load_h(j0, j0 + 8)
        bias_all = keep.tile([P, BRANCHES, H], BF16)
        nc.scalar.dma_start(
            out=bias_all[:].rearrange("p l o -> p (l o)"),
            in_=b_liq.rearrange("l o -> (l o)").partition_broadcast(P),
        )
        right_rows = keep.tile([P, H], BF16)
        nc.vector.memset(right_rows[:], 0.0)
        for i in range(TERMS):
            nc.scalar.dma_start(out=right_rows[i * BRANCHES : (i + 1) * BRANCHES, :], in_=g_liq)
        nc.scalar.dma_start(
            out=right_rows[TERMS * BRANCHES : (TERMS + 1) * BRANCHES, :], in_=beta_liq
        )
        g_row = keep.tile([P, BRANCHES, H], BF16)
        nc.vector.memset(g_row[:], 0.0)
        nc.scalar.dma_start(out=g_row[0:1, :, :], in_=g_liq.unsqueeze(0))

        ident = keep.tile([P, P], F32)
        make_identity(nc, ident[:])
        ident_bf = keep.tile([P, P], BF16)
        nc.vector.tensor_copy(out=ident_bf[:], in_=ident[:])
        ones = keep.tile([P, P], BF16)
        nc.vector.memset(ones[:], 1.0)
        eps = keep.tile([P, 1], F32)
        nc.vector.memset(eps[:], LN_EPS)
        left = keep.tile([P, 2, QUAD, P], BF16)
        nc.vector.memset(left[:], 0.0)
        nc.vector.memset(left[:, :, :, TERMS * BRANCHES : (TERMS + 1) * BRANCHES], -1.0 * H)

        first = keep.tile([P, 1], F32)
        nc.scalar.activation(out=first[:], in_=eps[:], func=ACT.Abs_reciprocal_sqrt)

        w_words = w_rows[:].bitcast(F32)
        w_codes = keep.tile([P, BRANCHES, H], U32, align_bytes=64)
        w_scales = keep.tile([P, BRANCHES, H], U8, align_bytes=64)
        w_grouped = {}

        def group_weights(l, copies):
            grouped_l = pairs.tile([P, H, 4], BF16, align_bytes=64)
            w_grouped[l] = grouped_l
            grouped_words = grouped_l[:].bitcast(F32)
            if l == 1:
                banks = []
                for half in range(2):
                    lin = prod.tile([P, H], F32)
                    banks.append(lin)
            else:
                total = turn.tile([P, H], F32)
                back = turn.tile([P, H], F32)
                banks = [total, back]
            for half, bank in enumerate(banks):
                w_bank = bank[:].rearrange("p (u o) -> p u o", u=2)
                for c in range(2):
                    transpose_words(
                        nc, w_bank, c * P, w_words[:, l * CHUNKS + 2 * half + c, :], ident
                    )
                copies[half](
                    out=grouped_words[:, half * 2 * P : (half + 1) * 2 * P, :],
                    in_=w_bank.rearrange("p u o -> p o u"),
                )

        def quantise_weights(l):
            nc.vector.quantize_mx(
                out=w_codes[:, l, :].bitcast(FP8X4),
                scales=w_scales[:, l, :],
                in_=w_grouped[l][:].rearrange("p o t -> p (o t)"),
            )

        h_words = h_rows[:].bitcast(F32)
        h_codes = keep.tile([P, TILES * P], U32, align_bytes=64)
        h_scales = keep.tile([P, TILES * P], U8, align_bytes=64)
        grouped = {}

        turned_words = {}

        def flip_two_tiles(j0):
            bank = flip.tile([P, H], F32)
            h_bank = bank[:].rearrange("p (u r) -> p u r", u=2)
            for c in range(2):
                transpose_words(nc, h_bank, c * P, h_words[:, j0 + c, :], ident)
            turned_words[j0] = h_bank

        def group_two_tiles(j0, copy):
            batch = [b for b in BATCHES if b[0] <= j0 < b[1]][0]
            if j0 == batch[0]:
                h_grouped = pairs.tile([P, 8 * P, 4], BF16, align_bytes=64)
                grouped[batch] = h_grouped
            r0 = (j0 - batch[0]) * P
            copy(
                out=grouped[batch][:, r0 : r0 + 2 * P, :].bitcast(F32),
                in_=turned_words[j0].rearrange("p u r -> p r u"),
            )

        def quantise_batch(batch):
            j0, j1 = batch
            nc.vector.quantize_mx(
                out=h_codes[:, j0 * P : j1 * P].bitcast(FP8X4),
                scales=h_scales[:, j0 * P : j1 * P],
                in_=grouped[batch][:, 0 : (j1 - j0) * P, :].rearrange("p r t -> p (r t)"),
            )

        products = {}
        resids = {}
        pres = {}
        row_sums = {}
        sq_sums = {}
        inv_stds = {}
        offs = {}
        rests = {}
        lefts = {}
        sums = {}
        turned = {}

        def residual(j):
            resid = quads.tile([P, BRANCHES, H], F32)
            step = 1 if j < 3 else BRANCHES
            for l in range(0, BRANCHES, step):
                nc.gpsimd.tensor_tensor(
                    out=resid[:, l : l + step, :],
                    in0=h_rows[:, j, :].unsqueeze(1).to_broadcast([P, step, H]),
                    in1=bias_all[:, l : l + step, :],
                    op=ALU.add,
                )
            resids[j] = resid

        def multiply(j, l):
            lin = prod.tile([P, H], F32)
            for again in range(PASSES[l]):
                nc.tensor.matmul_mx(
                    out=lin[:],
                    lhsT=h_codes[:, j * P : (j + 1) * P].bitcast(FP8X4),
                    lhsT_scale=h_scales[:, j * P : (j + 1) * P],
                    rhs=w_codes[:, l, :].bitcast(FP8X4),
                    rhs_scale=w_scales[:, l, :],
                    start=True,
                    stop=True,
                )
            products[j, l] = lin

        def add_residual(j, l):
            s, q = j // QUAD, j % QUAD
            if l == 0:
                pre = fives.tile([P, BRANCHES, H], F32)
                pres[j] = pre
                if q == 0:
                    row_sum = triples.tile([P, QUAD, BRANCHES], F32)
                    row_sums[s] = row_sum
            nc.vector.scalar_tensor_tensor(
                out=pres[j][:, l, :],
                in0=products[j, l][:],
                scalar=0.0,
                in1=resids[j][:, l, :],
                op0=ALU.add,
                op1=ALU.add,
                accum_out=row_sums[s][:, q, l : l + 1],
            )

        def deviation(j):
            s, q = j // QUAD, j % QUAD
            if q == 0:
                inv_std = pairs.tile([P, QUAD, BRANCHES], F32)
                inv_stds[s] = inv_std
            sq_sum = small.tile([P, BRANCHES], F32)
            for l in range(BRANCHES):
                squares = pairs.tile([P, H], F32)
                nc.scalar.activation(
                    out=squares[:],
                    in_=pres[j][:, l, :],
                    func=ACT.Square,
                    bias=row_sums[s][:, q, l : l + 1],
                    scale=-1.0 * H,
                    accum_out=sq_sum[:, l : l + 1],
                )
            sq_sums[j] = sq_sum

        def inverse(j):
            s, q = j // QUAD, j % QUAD
            nc.scalar.activation(
                out=inv_stds[s][:, q, :],
                in_=sq_sums[j][:],
                func=ACT.Abs_reciprocal_sqrt,
                bias=eps[:],
                scale=1.0 / H**3,
            )

        def first_term(s):
            offset = pairs.tile([P, QUAD, BRANCHES], F32)
            offs[s] = offset
            nc.vector.tensor_tensor(
                out=offset[:], in0=row_sums[s][:], in1=inv_stds[s][:], op=ALU.mult
            )

        def place_first_term(s):
            nc.scalar.copy(out=left[:, s % 2, :, 0:3], in_=offs[s][:])

        def second_term(s):
            slot = left[:, s % 2, :, :]
            rest = pairs.tile([P, QUAD, BRANCHES], F32)
            rests[s] = rest
            nc.vector.tensor_tensor(
                out=rest[:], in0=offs[s][:], in1=slot[:, :, 0:3], op=ALU.subtract
            )

        def place_second_term(s):
            nc.scalar.copy(out=left[:, s % 2, :, 3:6], in_=rests[s][:])

        def third_term(s):
            slot = left[:, s % 2, :, :]
            nc.vector.tensor_tensor(
                out=slot[:, :, 6:9], in0=rests[s][:], in1=slot[:, :, 3:6], op=ALU.subtract
            )

        def turn_left(s):
            left_bank = flip.tile([P, QUAD * P], BF16, tag="bank")
            for i in range(QUAD):
                nc.tensor.transpose(
                    left_bank[:, i * P : (i + 1) * P], left[:, s % 2, i, :], ident_bf[:]
                )
            left_turned = pairs.tile([P, QUAD * P], BF16)
            nc.scalar.copy(out=left_turned[:], in_=left_bank[:])
            lefts[s] = left_turned

        def scale(j, l):
            pre = pres[j]
            nc.vector.scalar_tensor_tensor(
                out=pre[:, l, :],
                in0=pre[:, l, :],
                scalar=inv_stds[j // QUAD][:, j % QUAD, l : l + 1],
                in1=gains[l],
                op0=ALU.mult,
                op1=ALU.mult,
            )

        def sum_branches(j, branches):
            pre = pres[j]
            if 0 in branches:
                if j < TILES - SUM_LAG:
                    total = turn.tile([P, H], F32)
                    sums[j] = total
                else:
                    lin = prod.tile([P, H], F32)
                    sums[j] = lin
            for l in branches:
                for c in range(CHUNKS):
                    nc.tensor.matmul(
                        sums[j][:, c * P : (c + 1) * P],
                        lhsT=pre[:, l, c * P : (c + 1) * P],
                        rhs=ident[:],
                        is_transpose=True,
                        start=(l == 0 and c == 0),
                        stop=(l == BRANCHES - 1 and c == CHUNKS - 1),
                    )

        def take_sum(j, copy):
            total_sb = eights.tile([P, H], F32)
            copy(out=total_sb[:], in_=sums[j][:])
            turned[j] = total_sb

        backs = {}

        def turn_back(j):
            if j < TILES - BACK_LAG or j % 3 == 0:
                back = turn.tile([P, H], F32)
                bank = back
            elif j % 3 == 1:
                total = turn.tile([P, H], F32)
                bank = total
            else:
                lin = prod.tile([P, H], F32)
                bank = lin
            nc.tensor.matmul(
                bank[:],
                lhsT=lefts[j // QUAD][:, (j % QUAD) * P : (j % QUAD + 1) * P],
                rhs=right[:],
                start=True,
                stop=False,
            )
            for c in range(CHUNKS):
                nc.tensor.matmul(
                    bank[:, c * P : (c + 1) * P],
                    lhsT=turned[j][:, c * P : (c + 1) * P],
                    rhs=ident[:],
                    is_transpose=True,
                    start=False,
                    stop=(c == CHUNKS - 1),
                )
            backs[j] = bank

        def add_branches(j):
            direct = quads.tile([P, H], F32)
            nc.vector.tensor_tensor(
                out=direct[:], in0=pres[j][:, 0, :], in1=pres[j][:, 1, :], op=ALU.add
            )
            nc.vector.tensor_tensor(
                out=direct[:], in0=direct[:], in1=pres[j][:, 2, :], op=ALU.add
            )
            turned[j] = direct

        def correct(j):
            lin = prod.tile([P, H], F32)
            nc.tensor.matmul(
                lin[:],
                lhsT=lefts[j // QUAD][:, (j % QUAD) * P : (j % QUAD + 1) * P],
                rhs=right[:],
                start=True,
                stop=True,
            )
            backs[j] = lin

        def store_direct(j):
            result = eights.tile([P, H], F32)
            nc.vector.tensor_tensor(
                out=result[:], in0=backs[j][:], in1=turned[j][:], op=ALU.add
            )
            nc.sync.dma_start(out=out_view[:, j, :], in_=result[:])

        def store(j, copy):
            result = eights.tile([P, H], F32)
            copy(out=result[:], in_=backs[j][:])
            nc.sync.dma_start(out=out_view[:, j, :], in_=result[:])

        residual(0)
        residual(1)
        flip_two_tiles(0)
        group_two_tiles(0, nc.vector.tensor_copy)
        group_weights(0, (nc.scalar.copy, nc.vector.tensor_copy))
        quantise_batch(BATCHES[0])
        quantise_weights(0)
        group_weights(1, (nc.scalar.copy, nc.vector.tensor_copy))
        multiply(0, 0)
        quantise_weights(1)
        add_residual(0, 0)
        group_weights(2, (nc.scalar.copy, nc.vector.tensor_copy))
        multiply(0, 1)
        quantise_weights(2)
        add_residual(0, 1)
        for j0 in range(2, GROUPED, 2):
            flip_two_tiles(j0)
            group_two_tiles(j0, nc.scalar.copy)
        multiply(0, 2)
        add_residual(0, 2)
        right = keep.tile([P, H], BF16)
        nc.vector.tensor_scalar(
            out=right[:], in0=right_rows[:], scalar1=-1.0 / H, scalar2=None, op0=ALU.mult
        )
        gain_a = gain.tile([P, 2, H], BF16)
        gain_b = gain.tile([P, 2, H], BF16)
        gains = [gain_a[:, 0, :], gain_a[:, 1, :], gain_b[:, 0, :]]

        for t in range(TILES):
            for l in range(BRANCHES):
                if t >= 1:
                    add_residual(t, l)
                if l == BRANCHES - 1:
                    for batch in BATCHES[1:]:
                        if t == max(batch[0] - 2, 0):
                            quantise_batch(batch)
                    if t % QUAD == 1 and t > QUAD:
                        first_term(t // QUAD - 1)
                    if t % QUAD == 2 and t > QUAD:
                        second_term(t // QUAD - 1)
                    if t % QUAD == 3 and t > QUAD:
                        third_term(t // QUAD - 1)
                if t >= SCALE_LAG:
                    scale(t - SCALE_LAG, l)
                if t + 1 < TILES:
                    multiply(t + 1, l)
                if t == 0:
                    nc.tensor.matmul(
                        gains[l], lhsT=ones[:], rhs=g_row[:, l, :], start=True, stop=True
                    )
                if l == 0:
                    if t >= SUM_LAG:
                        sum_branches(t - SUM_LAG, range(BRANCHES))
                    if t >= BACK_LAG:
                        turn_back(t - BACK_LAG)
                    for j0 in range(GROUPED, TILES, 2):
                        if t == max(j0 // 2 - 2, j0 - 9):
                            flip_two_tiles(j0)
            if t + 2 < TILES:
                residual(t + 2)
            if t >= 1:
                deviation(t - 1)
            if SUM_LAG <= t < TILES - 1:
                take_sum(t - SUM_LAG, nc.scalar.copy)
            if t >= 1:
                inverse(t - 1)
            if t % QUAD == 1 and t > QUAD:
                place_first_term(t // QUAD - 1)
            if t % QUAD == 2 and t > QUAD:
                place_second_term(t // QUAD - 1)
            if t >= BACK_LAG:
                store(t - BACK_LAG, nc.scalar.copy)
            for j0 in range(GROUPED, TILES, 2):
                if t == max(j0 // 2 - 2, j0 - 9):
                    group_two_tiles(j0, nc.scalar.copy)
            if t % QUAD == 3 and t > QUAD:
                turn_left(t // QUAD - 1)

        last = TILES - 1
        deviation(last)
        sum_branches(last - 2, range(BRANCHES))
        take_sum(last - 3, nc.scalar.copy)
        inverse(last)
        turn_back(last - 7)
        for l in range(BRANCHES):
            scale(last - 1, l)
        add_branches(last - 1)
        take_sum(last - 2, nc.scalar.copy)
        turn_back(last - 6)
        first_term(last // QUAD)
        place_first_term(last // QUAD)
        second_term(last // QUAD)
        place_second_term(last // QUAD)
        for l in range(BRANCHES):
            scale(last, l)
        third_term(last // QUAD)
        turn_left(last // QUAD)
        add_branches(last)
        store(last - 7, nc.scalar.copy)
        store(last - 6, nc.scalar.copy)
        turn_back(last - 5)
        turn_back(last - 4)
        correct(last - 1)
        correct(last)
        store(last - 5, nc.scalar.copy)
        store_direct(last - 1)
        store_direct(last)
        turn_back(last - 3)
        store(last - 4, nc.scalar.copy)
        turn_back(last - 2)
        store(last - 3, nc.vector.tensor_copy)
        store(last - 2, nc.scalar.copy)
